import numpy as np
import ml_dtypes


def mxq(x, axis, fmt="e4m3"):
    dtype, down = {"e4m3": (ml_dtypes.float8_e4m3fn, 7), "e5m2": (ml_dtypes.float8_e5m2, 14)}[fmt]
    v = np.moveaxis(np.asarray(x, np.float32).astype(ml_dtypes.bfloat16).astype(np.float64), axis, -1)
    blocks = v.reshape(v.shape[:-1] + (-1, 32))
    amax = np.abs(blocks).max(-1, keepdims=True)
    byte = np.maximum(np.where(amax > 0, np.frexp(amax)[1] - 1 + 127, 0) - down, 1)
    scale = np.exp2(byte - 127.0)
    codes = (blocks / scale).astype(np.float32).astype(dtype).astype(np.float64)
    return np.moveaxis((codes * scale).reshape(v.shape), -1, axis)


WIDE = False


def mx_kscale(k):
    if not WIDE:
        return np.ones(k)
    levels = np.array([10, -10, 5, -5, 0])
    a = np.random.permutation(np.resize(levels, k // 512 * 4)).reshape(k // 512, 4)
    idx = np.arange(k)
    return np.exp2(a[idx // 512, idx % 128 // 32])


BF16 = ml_dtypes.bfloat16


def bf(x):
    return np.asarray(x, np.float32).astype(BF16)


def f64(x):
    return np.asarray(x).astype(np.float64)


E2M1 = np.array([0.0, 0.5, 1.0, 1.5, 2.0, 3.0, 4.0, 6.0, -0.0, -0.5, -1.0, -1.5, -2.0, -3.0, -4.0, -6.0])


def pack_weight(w, fmt):
    k, n = w.shape
    w = f64(bf(w)).reshape(k // 32, 32, n)
    amax = np.abs(w).max(1)
    if fmt == "e4m3":
        byte = np.frexp(amax)[1] - 1 + 127 - 7
    else:
        mant, ex = np.frexp(amax / 6.0)
        byte = np.where(mant > 0.5, ex, ex - 1) + 127
    byte = np.clip(np.where(amax > 0, byte, 1), 1, 254)
    scaled = (w * np.exp2(127.0 - byte)[:, None, :]).reshape(k, n).astype(np.float32)
    by_word = np.ascontiguousarray(scaled.reshape(k // 512, 128, 4, n).transpose(0, 1, 3, 2))
    if fmt == "e4m3":
        words = by_word.astype(ml_dtypes.float8_e4m3fn).view(np.uint8)
    else:
        c = by_word.astype(ml_dtypes.float4_e2m1fn).view(np.uint8) & 0xF
        words = c[..., 0::2] | (c[..., 1::2] << 4)
    return np.ascontiguousarray(words), np.ascontiguousarray(byte.astype(np.uint8).reshape(k // 512, 16, n))


def unpack_weight(words, scales, fmt):
    g, p, n, _ = words.shape
    if fmt == "e4m3":
        vals = np.ascontiguousarray(words).view(ml_dtypes.float8_e4m3fn).astype(np.float64)
    else:
        nib = np.empty((g, p, n, 4), np.uint8)
        nib[..., 0::2] = words & 0xF
        nib[..., 1::2] = words >> 4
        vals = E2M1[nib]
    vals = vals * np.repeat(np.exp2(scales.astype(np.float64) - 127.0), 8, axis=1)[..., None]
    return vals.transpose(0, 1, 3, 2).reshape(g * 512, n)


B, K, N = 2048, 1024, 1024
EPS = 1e-7
MIN_NORM = 1e-15
MAX_TANH_ARG = 15.0


def _cosh(v):
    return 0.5 * (np.exp(v) + np.exp(-v))


def _sinh(v):
    return 0.5 * (np.exp(v) - np.exp(-v))


def _arccosh(v):
    return np.log(v + np.sqrt(v * v - 1.0))


def _norm(v):
    return np.sqrt(np.sum(v * v, axis=-1, keepdims=True))


def _mink_dot(u, v):
    return -u[..., :1] * v[..., :1] + np.sum(u[..., 1:] * v[..., 1:], axis=-1, keepdims=True)


def _proj(x):
    sp = x[..., 1:]
    t = np.sqrt(1.0 + np.sum(sp * sp, axis=-1, keepdims=True))
    return np.concatenate([t, sp], axis=-1)


def _proj_tan(u, x):
    ux = np.sum(x[..., 1:] * u[..., 1:], axis=-1, keepdims=True)
    t = ux / np.maximum(x[..., :1], MIN_NORM)
    return np.concatenate([t, u[..., 1:]], axis=-1)


def logmap_0(x):
    sp = x[..., 1:]
    n = np.maximum(_norm(sp), MIN_NORM)
    theta = np.maximum(x[..., :1], 1.0 + EPS)
    out_sp = _arccosh(theta) * sp / n
    return np.concatenate([np.zeros_like(theta), out_sp], axis=-1)


def expmap_0(u, backproject=True):
    sp = u[..., 1:]
    n = np.maximum(_norm(sp), MIN_NORM)
    theta = np.minimum(n, MAX_TANH_ARG)
    t = _cosh(theta)
    out_sp = _sinh(theta) * sp / n
    res = np.concatenate([t, out_sp], axis=-1)
    return _proj(res) if backproject else res


def ptransp_0(u, x):
    x0 = x[..., :1]
    y = x[..., 1:]
    y_norm = np.maximum(_norm(y), MIN_NORM)
    y_hat = y / y_norm
    v_time = -y_norm
    v_space = (1.0 - x0) * y_hat
    alpha = np.sum(y_hat * u[..., 1:], axis=-1, keepdims=True)
    res_time = np.zeros_like(x0) - alpha * v_time
    res_space = u[..., 1:] - alpha * v_space
    res = np.concatenate([res_time, res_space], axis=-1)
    return _proj_tan(res, x)


def expmap(u, x, backproject=True):
    unorm = np.sqrt(np.maximum(_mink_dot(u, u), MIN_NORM))
    theta = np.minimum(np.maximum(unorm, MIN_NORM), MAX_TANH_ARG)
    res = _cosh(theta) * x + _sinh(theta) * u / theta
    return _proj(res) if backproject else res


def setup_inputs():
    s = mx_kscale(K)
    c = np.sqrt(np.mean(s * s))
    sp = (np.random.standard_normal((B, K)) + 1.0) * (4.0 / np.sqrt(2.0 * K)) * (0.5 + np.random.random((B, 1)))
    sp = sp * s[None, :] / c
    t = np.sqrt(1.0 + np.sum(sp * sp, axis=-1, keepdims=True))
    w0 = np.random.standard_normal((N, K)) * (0.8 / np.sqrt(N))
    p = w0.sum(axis=1)
    b = 0.5 * np.random.standard_normal((1, N)) / np.sqrt(N) + 0.5 * p[None, :] / np.sqrt(np.sum(p * p))
    words, scales = pack_weight((w0 / s[None, :] * c).T, "e4m3")
    return {"x": bf(np.concatenate([t, sp], axis=-1)), "weight_words": words, "weight_scales": scales, "bias": bf(b)}


def reference(x, weight_words, weight_scales, bias):
    x, bias = f64(x), f64(bias)
    u = logmap_0(x)
    h_sp = mxq(u[..., 1:], 1, "e4m3") @ unpack_weight(weight_words, weight_scales, "e4m3")
    h = np.concatenate([np.zeros_like(h_sp[..., :1]), h_sp], axis=-1)
    m = expmap_0(h, backproject=True)
    b = np.concatenate([np.zeros_like(bias[..., :1]), bias], axis=-1)
    b = np.broadcast_to(b, m.shape)
    pt_b = ptransp_0(b, m)
    return expmap(pt_b, m, backproject=True)

@@ -1,0 +1,250 @@
+from contextlib import ExitStack
+
+import concourse.mybir as mybir
+from concourse.masks import make_identity
+
+F32 = mybir.dt.float32
+BF16 = mybir.dt.bfloat16
+I32 = mybir.dt.int32
+U32 = mybir.dt.uint32
+U8 = mybir.dt.uint8
+FP8X4 = mybir.dt.float8_e4m3fn_x4
+ALU = mybir.AluOpType
+ACT = mybir.ActivationFunctionType
+
+P = 128
+ROWS = 2048
+K = 1024
+N = 1024
+K_PASS = 512
+PASSES = K // K_PASS
+BANK = 512
+HALVES = N // BANK
+TILES = ROWS // P
+GROUP = 4
+GROUPS = TILES // GROUP
+X_PITCH = 1040
+
+EPS = 1e-7
+MIN_SQ = 1e-30
+MAX_ARG = 15.0
+
+FLOPS = 2 * ROWS * K * N
+
+
+def multiply(nc, h_bank, u_codes, u_scales, w_codes, w_scales, i, nh):
+    n_cols = slice(nh * BANK, (nh + 1) * BANK)
+    for g in range(PASSES):
+        m_cols = slice(g * P, (g + 1) * P)
+        nc.tensor.matmul_mx(
+            out=h_bank[:],
+            lhsT=u_codes[:, i, m_cols].bitcast(FP8X4),
+            lhsT_scale=u_scales[:, i, m_cols],
+            rhs=w_codes[:, g, n_cols].bitcast(FP8X4),
+            rhs_scale=w_scales[:, g, n_cols],
+            start=(g == 0),
+            stop=(g == PASSES - 1),
+        )
+
+
+def tile_hyperboliclinearhyperboloid_kernel(tc, x, weight_words, weight_scales, bias, out):
+    nc = tc.nc
+    with ExitStack() as ctx:
+        keep = ctx.enter_context(tc.tile_pool(name="keep", bufs=1))
+        work = ctx.enter_context(tc.tile_pool(name="work", bufs=3))
+        small = ctx.enter_context(tc.tile_pool(name="small", bufs=4))
+        turn = ctx.enter_context(tc.psum_pool(name="turn", bufs=2))
+        sums = ctx.enter_context(tc.psum_pool(name="sums", bufs=3))
+
+        ident = keep.tile([P, P], F32)
+        make_identity(nc, ident[:])
+        half = keep.tile([P, TILES], F32)
+        nc.vector.memset(half[:], 0.5)
+        neg_half = keep.tile([P, GROUP], F32)
+        nc.vector.memset(neg_half[:], -0.5)
+
+        w_codes = keep.tile([P, PASSES, N], U32, align_bytes=64)
+        w_scales = keep.tile([P, PASSES, N], U8, align_bytes=64)
+        nc.vector.memset(w_scales[:].rearrange("p g n -> p (g n)").bitcast(I32), 0)
+
+        x_all = keep.tile([P, TILES, X_PITCH], BF16)
+        x_time = keep.tile([P, TILES], BF16)
+        with nc.allow_non_contiguous_dma(reason="one bfloat16 element of each row of x"):
+            nc.sync.dma_start(out=x_time[:], in_=x[:, 0:1].rearrange("(i p) o -> p (i o)", p=P))
+        for i in range(GROUP):
+            nc.sync.dma_start(out=x_all[:, i, 0:K], in_=x[i * P : (i + 1) * P, 1 : K + 1])
+        for g in range(PASSES):
+            nc.sync.dma_start(
+                out=w_codes[:, g, :].bitcast(I32),
+                in_=weight_words[g].rearrange("p n t -> p (n t)").bitcast(I32),
+            )
+        for g in range(PASSES):
+            for quad in range(4):
+                nc.sync.dma_start(
+                    out=w_scales[32 * quad : 32 * quad + 4, g, :].bitcast(I32),
+                    in_=weight_scales[g, 4 * quad : 4 * quad + 4, :].bitcast(I32),
+                )
+        b_rows = keep.tile([P, N], BF16)
+        nc.sync.dma_start(out=b_rows[:], in_=bias.rearrange("o n -> (o n)").partition_broadcast(P))
+        for i in range(GROUP, TILES):
+            nc.sync.dma_start(out=x_all[:, i, 0:K], in_=x[i * P : (i + 1) * P, 1 : K + 1])
+
+        u_codes = keep.tile([P, TILES, PASSES * P], U32, align_bytes=64)
+        u_scales = keep.tile([P, TILES, PASSES * P], U8, align_bytes=64)
+
+        theta = keep.tile([P, TILES], F32)
+        nc.vector.tensor_scalar(out=theta[:], in0=x_time[:], scalar1=1.0 + EPS, scalar2=None, op0=ALU.max)
+        theta_less = keep.tile([P, TILES], F32)
+        nc.vector.tensor_scalar(out=theta_less[:], in0=theta[:], scalar1=-1.0, scalar2=None, op0=ALU.add)
+        below = keep.tile([P, TILES], F32)
+        nc.vector.scalar_tensor_tensor(
+            out=below[:], in0=theta[:], scalar=1.0, in1=theta_less[:], op0=ALU.add, op1=ALU.mult
+        )
+        root = keep.tile([P, TILES], F32)
+        nc.gpsimd.tensor_tensor(out=root[:], in0=below[:], in1=half[:], op=ALU.pow)
+        ln_arg = keep.tile([P, TILES], F32)
+        nc.vector.tensor_tensor(out=ln_arg[:], in0=theta[:], in1=root[:], op=ALU.add)
+        dist = keep.tile([P, TILES], F32)
+        nc.scalar.activation(out=dist[:], in_=ln_arg[:], func=ACT.Ln)
+
+        b_junk = work.tile([P, N], BF16)
+        b_sq = keep.tile([P, 1], F32)
+        nc.scalar.activation(out=b_junk[:], in_=b_rows[:], func=ACT.Square, accum_out=b_sq[:])
+        b_sq_min = keep.tile([P, 1], F32)
+        nc.gpsimd.tensor_scalar(out=b_sq_min[:], in0=b_sq[:], scalar1=1e-15, scalar2=None, op0=ALU.max)
+        t_raw = keep.tile([P, 1], F32)
+        nc.gpsimd.tensor_tensor(out=t_raw[:], in0=b_sq_min[:], in1=half[:, 0:1], op=ALU.pow)
+        t_arg = keep.tile([P, 1], F32)
+        nc.gpsimd.tensor_scalar(out=t_arg[:], in0=t_raw[:], scalar1=1e-15, scalar2=MAX_ARG, op0=ALU.max, op1=ALU.min)
+        t_exp = keep.tile([P, 1], F32)
+        nc.scalar.activation(out=t_exp[:], in_=t_arg[:], func=ACT.Exp)
+        t_exp_neg = keep.tile([P, 1], F32)
+        nc.scalar.activation(out=t_exp_neg[:], in_=t_arg[:], func=ACT.Exp, scale=-1.0)
+        t_inv = keep.tile([P, 1], F32)
+        nc.vector.reciprocal(out=t_inv[:], in_=t_arg[:])
+        cosh_sum = keep.tile([P, 1], F32)
+        nc.gpsimd.tensor_tensor(out=cosh_sum[:], in0=t_exp[:], in1=t_exp_neg[:], op=ALU.add)
+        sinh_diff = keep.tile([P, 1], F32)
+        nc.gpsimd.tensor_tensor(out=sinh_diff[:], in0=t_exp[:], in1=t_exp_neg[:], op=ALU.subtract)
+        two_st = keep.tile([P, 1], F32)
+        nc.gpsimd.tensor_tensor(out=two_st[:], in0=sinh_diff[:], in1=t_inv[:], op=ALU.mult)
+        st = keep.tile([P, 1], F32)
+        nc.gpsimd.tensor_scalar(out=st[:], in0=two_st[:], scalar1=0.5, scalar2=None, op0=ALU.mult)
+        half_st = keep.tile([P, 1], F32)
+        nc.gpsimd.tensor_scalar(out=half_st[:], in0=two_st[:], scalar1=0.25, scalar2=None, op0=ALU.mult)
+        half_ct = keep.tile([P, 1], F32)
+        nc.gpsimd.tensor_scalar(out=half_ct[:], in0=cosh_sum[:], scalar1=0.25, scalar2=None, op0=ALU.mult)
+        st_sq = keep.tile([P, 1], F32)
+        nc.gpsimd.tensor_tensor(out=st_sq[:], in0=st[:], in1=st[:], op=ALU.mult)
+        st_sq_bb = keep.tile([P, 1], F32)
+        nc.gpsimd.tensor_tensor(out=st_sq_bb[:], in0=st_sq[:], in1=b_sq[:], op=ALU.mult)
+        one_plus = keep.tile([P, 1], F32)
+        nc.gpsimd.tensor_scalar(out=one_plus[:], in0=st_sq_bb[:], scalar1=1.0, scalar2=None, op0=ALU.add)
+        b_term = keep.tile([P, N], F32)
+        nc.vector.tensor_scalar(out=b_term[:], in0=b_rows[:], scalar1=st[:, 0:1], scalar2=None, op0=ALU.mult)
+
+        for grp in range(GROUPS):
+            h_sq_parts = small.tile([P, GROUP, HALVES], F32)
+            h_b_parts = small.tile([P, GROUP, HALVES], F32)
+            for j in range(GROUP):
+                i = grp * GROUP + j
+                sp = x_all[:, i, 0:K]
+                sq_junk = work.tile([P, K], BF16)
+                sp_sq = small.tile([P, 1], F32)
+                nc.scalar.activation(out=sq_junk[:], in_=sp, func=ACT.Square, accum_out=sp_sq[:])
+                sp_sq_min = small.tile([P, 1], F32)
+                nc.gpsimd.tensor_scalar(out=sp_sq_min[:], in0=sp_sq[:], scalar1=MIN_SQ, scalar2=None, op0=ALU.max)
+                inv_norm = small.tile([P, 1], F32)
+                nc.gpsimd.tensor_tensor(out=inv_norm[:], in0=sp_sq_min[:], in1=neg_half[:, 0:1], op=ALU.pow)
+                row_scale = small.tile([P, 1], F32)
+                nc.gpsimd.tensor_tensor(out=row_scale[:], in0=dist[:, i : i + 1], in1=inv_norm[:], op=ALU.mult)
+                u_bf = work.tile([P, K], BF16, align_bytes=64)
+                nc.vector.tensor_scalar(out=u_bf[:], in0=sp, scalar1=row_scale[:, 0:1], scalar2=None, op0=ALU.mult)
+
+                turned = turn.tile([P, PASSES, 2, P], F32)
+                u_words = u_bf[:].bitcast(F32)
+                for g in range(PASSES):
+                    for w in range(2):
+                        nc.tensor.transpose(turned[:, g, w, :], u_words[:, 256 * g + w : 256 * (g + 1) : 2], ident[:])
+                grouped = work.tile([P, PASSES * P * 4], BF16, align_bytes=64)
+                nc.scalar.copy(
+                    out=grouped[:].bitcast(F32).rearrange("p (g r w) -> p g r w", g=PASSES, w=2),
+                    in_=turned[:].rearrange("p g w r -> p g r w"),
+                )
+                nc.vector.quantize_mx(out=u_codes[:, i, :].bitcast(FP8X4), scales=u_scales[:, i, :], in_=grouped[:])
+
+                for nh in range(HALVES):
+                    h_bank = sums.tile([P, BANK], F32)
+                    multiply(nc, h_bank, u_codes, u_scales, w_codes, w_scales, i, nh)
+                    hh_junk = work.tile([P, BANK], BF16)
+                    nc.scalar.activation(
+                        out=hh_junk[:], in_=h_bank[:], func=ACT.Square, accum_out=h_sq_parts[:, j, nh : nh + 1]
+                    )
+                    hb_junk = work.tile([P, BANK], F32)
+                    nc.vector.scalar_tensor_tensor(
+                        out=hb_junk[:], in0=h_bank[:], scalar=1.0, in1=b_rows[:, nh * BANK : (nh + 1) * BANK],
+                        op0=ALU.mult, op1=ALU.mult, accum_out=h_b_parts[:, j, nh : nh + 1],
+                    )
+
+            h_sq = small.tile([P, GROUP], F32)
+            nc.vector.scalar_tensor_tensor(
+                out=h_sq[:], in0=h_sq_parts[:, :, 0], scalar=MIN_SQ, in1=h_sq_parts[:, :, 1], op0=ALU.max, op1=ALU.add
+            )
+            h_b = small.tile([P, GROUP], F32)
+            nc.vector.tensor_tensor(out=h_b[:], in0=h_b_parts[:, :, 0], in1=h_b_parts[:, :, 1], op=ALU.add)
+            r_inv = small.tile([P, GROUP], F32)
+            nc.gpsimd.tensor_tensor(out=r_inv[:], in0=h_sq[:], in1=neg_half[:], op=ALU.pow)
+            r_len = small.tile([P, GROUP], F32)
+            nc.gpsimd.tensor_tensor(out=r_len[:], in0=h_sq[:], in1=r_inv[:], op=ALU.mult)
+            r_arg = small.tile([P, GROUP], F32)
+            nc.gpsimd.tensor_scalar(out=r_arg[:], in0=r_len[:], scalar1=MAX_ARG, scalar2=None, op0=ALU.min)
+            r_exp = small.tile([P, GROUP], F32)
+            nc.scalar.activation(out=r_exp[:], in_=r_arg[:], func=ACT.Exp)
+            r_exp_neg = small.tile([P, GROUP], F32)
+            nc.scalar.activation(out=r_exp_neg[:], in_=r_arg[:], func=ACT.Exp, scale=-1.0)
+            r_tanh = small.tile([P, GROUP], F32)
+            nc.scalar.activation(out=r_tanh[:], in_=r_arg[:], func=ACT.Tanh, scale=0.5)
+            along = small.tile([P, GROUP], F32)
+            nc.gpsimd.tensor_tensor(out=along[:], in0=h_b[:], in1=r_inv[:], op=ALU.mult)
+            two_sinh = small.tile([P, GROUP], F32)
+            nc.gpsimd.tensor_tensor(out=two_sinh[:], in0=r_exp[:], in1=r_exp_neg[:], op=ALU.subtract)
+            two_c1 = small.tile([P, GROUP], F32)
+            nc.gpsimd.tensor_tensor(out=two_c1[:], in0=two_sinh[:], in1=r_inv[:], op=ALU.mult)
+            lift = small.tile([P, GROUP], F32)
+            nc.gpsimd.tensor_tensor(out=lift[:], in0=r_tanh[:], in1=along[:], op=ALU.mult)
+            mix = small.tile([P, GROUP], F32)
+            nc.gpsimd.tensor_scalar(
+                out=mix[:], in0=lift[:], scalar1=half_st[:, 0:1], scalar2=half_ct[:, 0:1], op0=ALU.mult, op1=ALU.add
+            )
+            coef = small.tile([P, GROUP], F32)
+            nc.gpsimd.tensor_tensor(out=coef[:], in0=two_c1[:], in1=mix[:], op=ALU.mult)
+
+            cross = small.tile([P, GROUP], F32)
+            nc.gpsimd.tensor_scalar(out=cross[:], in0=h_b[:], scalar1=two_st[:, 0:1], scalar2=None, op0=ALU.mult)
+            o_sq_a = small.tile([P, GROUP], F32)
+            nc.gpsimd.tensor_tensor(out=o_sq_a[:], in0=coef[:], in1=h_sq[:], op=ALU.mult)
+            o_sq_b = small.tile([P, GROUP], F32)
+            nc.gpsimd.tensor_tensor(out=o_sq_b[:], in0=o_sq_a[:], in1=cross[:], op=ALU.add)
+            o_sq_c = small.tile([P, GROUP], F32)
+            nc.gpsimd.tensor_tensor(out=o_sq_c[:], in0=o_sq_b[:], in1=coef[:], op=ALU.mult)
+            time_sq = small.tile([P, GROUP], F32)
+            nc.gpsimd.tensor_scalar(out=time_sq[:], in0=o_sq_c[:], scalar1=one_plus[:, 0:1], scalar2=None, op0=ALU.add)
+            time_co = small.tile([P, GROUP], F32)
+            nc.gpsimd.tensor_tensor(out=time_co[:], in0=time_sq[:], in1=half[:, 0:GROUP], op=ALU.pow)
+
+            o_grp = work.tile([P, GROUP, N + 1], F32)
+            nc.vector.tensor_copy(out=o_grp[:, :, 0], in_=time_co[:])
+            for j in range(GROUP):
+                i = grp * GROUP + j
+                for nh in range(HALVES):
+                    o_bank = sums.tile([P, BANK], F32)
+                    multiply(nc, o_bank, u_codes, u_scales, w_codes, w_scales, i, nh)
+                    nc.vector.scalar_tensor_tensor(
+                        out=o_grp[:, j, 1 + nh * BANK : 1 + (nh + 1) * BANK],
+                        in0=o_bank[:],
+                        scalar=coef[:, j : j + 1],
+                        in1=b_term[:, nh * BANK : (nh + 1) * BANK],
+                        op0=ALU.mult,
+                        op1=ALU.add,
+                    )
+                nc.sync.dma_start(out=out[i * P : (i + 1) * P, :], in_=o_grp[:, j, :])

@@ -21,9 +21,7 @@ PASSES = K // K_PASS
 BANK = 512
 HALVES = N // BANK
 TILES = ROWS // P
-GROUP = 4
-GROUPS = TILES // GROUP
-X_PITCH = 1040
+O_PITCH = 1032
 
 EPS = 1e-7
 MIN_SQ = 1e-30
@@ -32,19 +30,8 @@ MAX_ARG = 15.0
 FLOPS = 2 * ROWS * K * N
 
 
-def multiply(nc, h_bank, u_codes, u_scales, w_codes, w_scales, i, nh):
-    n_cols = slice(nh * BANK, (nh + 1) * BANK)
-    for g in range(PASSES):
-        m_cols = slice(g * P, (g + 1) * P)
-        nc.tensor.matmul_mx(
-            out=h_bank[:],
-            lhsT=u_codes[:, i, m_cols].bitcast(FP8X4),
-            lhsT_scale=u_scales[:, i, m_cols],
-            rhs=w_codes[:, g, n_cols].bitcast(FP8X4),
-            rhs_scale=w_scales[:, g, n_cols],
-            start=(g == 0),
-            stop=(g == PASSES - 1),
-        )
+def col(tile, i):
+    return tile[:, i : i + 1]
 
 
 def tile_hyperboliclinearhyperboloid_kernel(tc, x, weight_words, weight_scales, bias, out):
@@ -52,27 +39,35 @@ def tile_hyperboliclinearhyperboloid_kernel(tc, x, weight_words, weight_scales, 
     with ExitStack() as ctx:
         keep = ctx.enter_context(tc.tile_pool(name="keep", bufs=1))
         work = ctx.enter_context(tc.tile_pool(name="work", bufs=3))
-        small = ctx.enter_context(tc.tile_pool(name="small", bufs=4))
+        junk = ctx.enter_context(tc.tile_pool(name="junk", bufs=2))
         turn = ctx.enter_context(tc.psum_pool(name="turn", bufs=2))
-        sums = ctx.enter_context(tc.psum_pool(name="sums", bufs=3))
+        prod = ctx.enter_context(tc.psum_pool(name="prod", bufs=6))
+        ctx.enter_context(tc.manual_schedule())
 
-        ident = keep.tile([P, P], F32)
-        make_identity(nc, ident[:])
         half = keep.tile([P, TILES], F32)
         nc.vector.memset(half[:], 0.5)
-        neg_half = keep.tile([P, GROUP], F32)
+        neg_half = keep.tile([P, TILES], F32)
         nc.vector.memset(neg_half[:], -0.5)
-
         w_codes = keep.tile([P, PASSES, N], U32, align_bytes=64)
         w_scales = keep.tile([P, PASSES, N], U8, align_bytes=64)
         nc.vector.memset(w_scales[:].rearrange("p g n -> p (g n)").bitcast(I32), 0)
+        ident = keep.tile([P, P], F32)
+        make_identity(nc, ident[:])
 
-        x_all = keep.tile([P, TILES, X_PITCH], BF16)
+        x_all = keep.tile([P, TILES, K], BF16)
         x_time = keep.tile([P, TILES], BF16)
+        b_rows = keep.tile([P, N], BF16)
+
+        def load_rows(i):
+            nc.sync.dma_start(out=x_all[:, i, :], in_=x[i * P : (i + 1) * P, 1 : K + 1])
+
         with nc.allow_non_contiguous_dma(reason="one bfloat16 element of each row of x"):
             nc.sync.dma_start(out=x_time[:], in_=x[:, 0:1].rearrange("(i p) o -> p (i o)", p=P))
-        for i in range(GROUP):
-            nc.sync.dma_start(out=x_all[:, i, 0:K], in_=x[i * P : (i + 1) * P, 1 : K + 1])
+        load_rows(0)
+        load_rows(1)
+        nc.sync.dma_start(out=b_rows[:], in_=bias.rearrange("o n -> (o n)").partition_broadcast(P))
+        load_rows(2)
+        load_rows(3)
         for g in range(PASSES):
             nc.sync.dma_start(
                 out=w_codes[:, g, :].bitcast(I32),
@@ -84,14 +79,184 @@ def tile_hyperboliclinearhyperboloid_kernel(tc, x, weight_words, weight_scales, 
                     out=w_scales[32 * quad : 32 * quad + 4, g, :].bitcast(I32),
                     in_=weight_scales[g, 4 * quad : 4 * quad + 4, :].bitcast(I32),
                 )
-        b_rows = keep.tile([P, N], BF16)
-        nc.sync.dma_start(out=b_rows[:], in_=bias.rearrange("o n -> (o n)").partition_broadcast(P))
-        for i in range(GROUP, TILES):
-            nc.sync.dma_start(out=x_all[:, i, 0:K], in_=x[i * P : (i + 1) * P, 1 : K + 1])
+        for i in range(4, TILES):
+            load_rows(i)
 
         u_codes = keep.tile([P, TILES, PASSES * P], U32, align_bytes=64)
         u_scales = keep.tile([P, TILES, PASSES * P], U8, align_bytes=64)
+        o_all = keep.tile([P, TILES, O_PITCH], F32)
 
+        sp_sq = keep.tile([P, TILES], F32)
+        sp_sq_min = keep.tile([P, TILES], F32)
+        inv_norm = keep.tile([P, TILES], F32)
+        h_sq_parts = keep.tile([P, TILES, HALVES], F32)
+        h_b_parts = keep.tile([P, TILES, HALVES], F32)
+        h_sq = keep.tile([P, TILES], F32)
+        r_inv = keep.tile([P, TILES], F32)
+        r_arg = keep.tile([P, TILES], F32)
+        along = keep.tile([P, TILES], F32)
+        x_fac = keep.tile([P, TILES], F32)
+        y_fac = keep.tile([P, TILES], F32)
+        shift = keep.tile([P, TILES], F32)
+        r_exp = keep.tile([P, TILES], F32)
+        r_exp_neg = keep.tile([P, TILES], F32)
+        y_neg = keep.tile([P, TILES], F32)
+        x_less_y = keep.tile([P, TILES], F32)
+        coef = keep.tile([P, TILES], F32)
+        z_sq = keep.tile([P, TILES], F32)
+        time_sq = keep.tile([P, TILES], F32)
+        time_co = keep.tile([P, TILES], F32)
+
+        u_of = {}
+        turned_of = {}
+        grouped_of = {}
+        bank_of = {}
+
+        def square_rows(i):
+            sp = x_all[:, i, :]
+            if i % 2 == 1 and i < 8:
+                sq_v = junk.tile([P, K], F32)
+                nc.vector.scalar_tensor_tensor(
+                    out=sq_v[:], in0=sp, scalar=1.0, in1=sp, op0=ALU.mult, op1=ALU.mult, accum_out=col(sp_sq, i)
+                )
+            else:
+                sq_s = junk.tile([P, K], BF16)
+                nc.scalar.activation(out=sq_s[:], in_=sp, func=ACT.Square, accum_out=col(sp_sq, i))
+
+        def inverse_norms(i, n):
+            cols = slice(i, i + n)
+            nc.gpsimd.tensor_scalar(out=sp_sq_min[:, cols], in0=sp_sq[:, cols], scalar1=MIN_SQ, scalar2=None, op0=ALU.max)
+            nc.gpsimd.tensor_tensor(out=inv_norm[:, cols], in0=sp_sq_min[:, cols], in1=neg_half[:, 0:n], op=ALU.pow)
+
+        def scale_rows(i):
+            u_bf = work.tile([P, K], BF16, align_bytes=64)
+            nc.vector.tensor_scalar(
+                out=u_bf[:], in0=x_all[:, i, :], scalar1=col(inv_norm, i), scalar2=col(dist, i), op0=ALU.mult, op1=ALU.mult
+            )
+            u_of[i] = u_bf
+
+        def turn_rows(i):
+            turned = turn.tile([P, PASSES, 2, P], F32)
+            u_words = u_of[i][:].bitcast(F32)
+            for g in range(PASSES):
+                for w in range(2):
+                    nc.tensor.transpose(turned[:, g, w, :], u_words[:, 256 * g + w : 256 * (g + 1) : 2], ident[:])
+            turned_of[i] = turned
+
+        def regroup(i):
+            grouped = work.tile([P, PASSES * P * 4], BF16, align_bytes=64)
+            nc.scalar.copy(
+                out=grouped[:].bitcast(F32).rearrange("p (g r w) -> p g r w", g=PASSES, w=2),
+                in_=turned_of[i][:].rearrange("p g w r -> p g r w"),
+            )
+            grouped_of[i] = grouped
+
+        def quantise(i):
+            nc.vector.quantize_mx(out=u_codes[:, i, :].bitcast(FP8X4), scales=u_scales[:, i, :], in_=grouped_of[i][:])
+
+        def multiply(i):
+            for nh in range(HALVES):
+                h_bank = prod.tile([P, BANK], F32)
+                n_cols = slice(nh * BANK, (nh + 1) * BANK)
+                for g in range(PASSES):
+                    m_cols = slice(g * P, (g + 1) * P)
+                    nc.tensor.matmul_mx(
+                        out=h_bank[:],
+                        lhsT=u_codes[:, i, m_cols].bitcast(FP8X4),
+                        lhsT_scale=u_scales[:, i, m_cols],
+                        rhs=w_codes[:, g, n_cols].bitcast(FP8X4),
+                        rhs_scale=w_scales[:, g, n_cols],
+                        start=(g == 0),
+                        stop=(g == PASSES - 1),
+                    )
+                bank_of[(i, nh)] = h_bank
+
+        def sum_h_bias(i, nh):
+            hb_junk = junk.tile([P, BANK], F32)
+            nc.vector.scalar_tensor_tensor(
+                out=hb_junk[:], in0=bank_of[(i, nh)][:], scalar=1.0, in1=b_rows[:, nh * BANK : (nh + 1) * BANK],
+                op0=ALU.mult, op1=ALU.mult, accum_out=h_b_parts[:, i, nh : nh + 1],
+            )
+
+        def sum_h_squared(i, nh):
+            hh_junk = junk.tile([P, BANK], BF16)
+            nc.scalar.activation(
+                out=hh_junk[:], in_=bank_of[(i, nh)][:], func=ACT.Square, accum_out=h_sq_parts[:, i, nh : nh + 1]
+            )
+
+        def chain_h_sq(i):
+            nc.vector.tensor_scalar(
+                out=col(h_sq, i), in0=h_sq_parts[:, i, 0:1], scalar1=h_sq_parts[:, i, 1:2], scalar2=MIN_SQ,
+                op0=ALU.add, op1=ALU.max,
+            )
+
+        def chain_r_inv(i):
+            nc.gpsimd.tensor_tensor(out=col(r_inv, i), in0=col(h_sq, i), in1=neg_half[:, 0:1], op=ALU.pow)
+
+        def chain_after_r_inv(i):
+            nc.vector.tensor_scalar(
+                out=col(r_arg, i), in0=col(h_sq, i), scalar1=col(r_inv, i), scalar2=MAX_ARG, op0=ALU.mult, op1=ALU.min
+            )
+            nc.vector.tensor_scalar(
+                out=col(along, i), in0=h_b_parts[:, i, 0:1], scalar1=h_b_parts[:, i, 1:2], scalar2=col(r_inv, i),
+                op0=ALU.add, op1=ALU.mult,
+            )
+            nc.vector.tensor_scalar(
+                out=col(shift, i), in0=col(along, i), scalar1=col(r_inv, i), scalar2=neg_st[:, 0:1],
+                op0=ALU.mult, op1=ALU.mult,
+            )
+
+        def exponentials(i):
+            nc.scalar.activation(out=col(r_exp, i), in_=col(r_arg, i), func=ACT.Exp)
+            nc.scalar.activation(out=col(r_exp_neg, i), in_=col(r_arg, i), func=ACT.Exp, scale=-1.0)
+            nc.scalar.activation(
+                out=col(y_fac, i), in_=col(along, i), func=ACT.Identity, scale=half_st[:, 0:1], bias=neg_half_ct[:, 0:1]
+            )
+            nc.scalar.activation(
+                out=col(x_fac, i), in_=col(along, i), func=ACT.Identity, scale=half_st[:, 0:1], bias=half_ct[:, 0:1]
+            )
+
+        def chain_y(i):
+            nc.scalar.activation(out=col(y_neg, i), in_=col(r_exp_neg, i), func=ACT.Identity, scale=col(y_fac, i))
+
+        def chain_x(i):
+            nc.scalar.activation(
+                out=col(x_less_y, i), in_=col(r_exp, i), func=ACT.Identity, scale=col(x_fac, i), bias=col(y_neg, i)
+            )
+
+        def chain_coef(i):
+            nc.scalar.activation(
+                out=col(coef, i), in_=col(x_less_y, i), func=ACT.Identity, scale=col(r_inv, i), bias=col(shift, i)
+            )
+            nc.scalar.activation(
+                out=col(z_sq, i), in_=col(y_neg, i), func=ACT.Square, scale=-2.0, bias=col(x_less_y, i)
+            )
+
+        def time_coordinates(i, n):
+            cols = slice(i, i + n)
+            nc.gpsimd.tensor_scalar(
+                out=time_sq[:, cols], in0=z_sq[:, cols], scalar1=delta[:, 0:1], scalar2=1.0, op0=ALU.add, op1=ALU.add
+            )
+            nc.gpsimd.tensor_tensor(out=time_co[:, cols], in0=time_sq[:, cols], in1=half[:, 0:n], op=ALU.pow)
+
+        def place_times(i, n):
+            nc.vector.tensor_copy(out=o_all[:, i : i + n, 0], in_=time_co[:, i : i + n])
+
+        def finish(i, nh):
+            nc.vector.scalar_tensor_tensor(
+                out=o_all[:, i, 1 + nh * BANK : 1 + (nh + 1) * BANK],
+                in0=bank_of[(i, nh)][:],
+                scalar=col(coef, i),
+                in1=b_term[:, nh * BANK : (nh + 1) * BANK],
+                op0=ALU.mult,
+                op1=ALU.add,
+            )
+
+        def store(i):
+            nc.sync.dma_start(out=out[i * P : (i + 1) * P, :], in_=o_all[:, i, 0 : N + 1])
+
+        warm = keep.tile([P, 2], F32)
+        nc.scalar.activation(out=warm[:, 0:1], in_=half[:, 0:1], func=ACT.Ln)
         theta = keep.tile([P, TILES], F32)
         nc.vector.tensor_scalar(out=theta[:], in0=x_time[:], scalar1=1.0 + EPS, scalar2=None, op0=ALU.max)
         theta_less = keep.tile([P, TILES], F32)
@@ -104,147 +269,132 @@ def tile_hyperboliclinearhyperboloid_kernel(tc, x, weight_words, weight_scales, 
         nc.gpsimd.tensor_tensor(out=root[:], in0=below[:], in1=half[:], op=ALU.pow)
         ln_arg = keep.tile([P, TILES], F32)
         nc.vector.tensor_tensor(out=ln_arg[:], in0=theta[:], in1=root[:], op=ALU.add)
+        square_rows(0)
+        square_rows(1)
         dist = keep.tile([P, TILES], F32)
         nc.scalar.activation(out=dist[:], in_=ln_arg[:], func=ACT.Ln)
+        nc.scalar.activation(out=warm[:, 1:2], in_=half[:, 0:1], func=ACT.Exp)
+        square_rows(2)
+        inverse_norms(0, 2)
 
-        b_junk = work.tile([P, N], BF16)
+        b_junk = junk.tile([P, N], F32)
         b_sq = keep.tile([P, 1], F32)
-        nc.scalar.activation(out=b_junk[:], in_=b_rows[:], func=ACT.Square, accum_out=b_sq[:])
+        nc.vector.scalar_tensor_tensor(
+            out=b_junk[:], in0=b_rows[:], scalar=1.0, in1=b_rows[:], op0=ALU.mult, op1=ALU.mult, accum_out=b_sq[:]
+        )
         b_sq_min = keep.tile([P, 1], F32)
-        nc.gpsimd.tensor_scalar(out=b_sq_min[:], in0=b_sq[:], scalar1=1e-15, scalar2=None, op0=ALU.max)
+        nc.vector.tensor_scalar(out=b_sq_min[:], in0=b_sq[:], scalar1=1e-15, scalar2=None, op0=ALU.max)
         t_raw = keep.tile([P, 1], F32)
         nc.gpsimd.tensor_tensor(out=t_raw[:], in0=b_sq_min[:], in1=half[:, 0:1], op=ALU.pow)
+        scale_rows(0)
+        scale_rows(1)
         t_arg = keep.tile([P, 1], F32)
-        nc.gpsimd.tensor_scalar(out=t_arg[:], in0=t_raw[:], scalar1=1e-15, scalar2=MAX_ARG, op0=ALU.max, op1=ALU.min)
+        nc.vector.tensor_scalar(out=t_arg[:], in0=t_raw[:], scalar1=1e-15, scalar2=MAX_ARG, op0=ALU.max, op1=ALU.min)
+        t_inv = keep.tile([P, 1], F32)
+        nc.vector.reciprocal(out=t_inv[:], in_=t_arg[:])
         t_exp = keep.tile([P, 1], F32)
         nc.scalar.activation(out=t_exp[:], in_=t_arg[:], func=ACT.Exp)
         t_exp_neg = keep.tile([P, 1], F32)
         nc.scalar.activation(out=t_exp_neg[:], in_=t_arg[:], func=ACT.Exp, scale=-1.0)
-        t_inv = keep.tile([P, 1], F32)
-        nc.vector.reciprocal(out=t_inv[:], in_=t_arg[:])
-        cosh_sum = keep.tile([P, 1], F32)
-        nc.gpsimd.tensor_tensor(out=cosh_sum[:], in0=t_exp[:], in1=t_exp_neg[:], op=ALU.add)
-        sinh_diff = keep.tile([P, 1], F32)
-        nc.gpsimd.tensor_tensor(out=sinh_diff[:], in0=t_exp[:], in1=t_exp_neg[:], op=ALU.subtract)
-        two_st = keep.tile([P, 1], F32)
-        nc.gpsimd.tensor_tensor(out=two_st[:], in0=sinh_diff[:], in1=t_inv[:], op=ALU.mult)
-        st = keep.tile([P, 1], F32)
-        nc.gpsimd.tensor_scalar(out=st[:], in0=two_st[:], scalar1=0.5, scalar2=None, op0=ALU.mult)
-        half_st = keep.tile([P, 1], F32)
-        nc.gpsimd.tensor_scalar(out=half_st[:], in0=two_st[:], scalar1=0.25, scalar2=None, op0=ALU.mult)
         half_ct = keep.tile([P, 1], F32)
-        nc.gpsimd.tensor_scalar(out=half_ct[:], in0=cosh_sum[:], scalar1=0.25, scalar2=None, op0=ALU.mult)
-        st_sq = keep.tile([P, 1], F32)
-        nc.gpsimd.tensor_tensor(out=st_sq[:], in0=st[:], in1=st[:], op=ALU.mult)
-        st_sq_bb = keep.tile([P, 1], F32)
-        nc.gpsimd.tensor_tensor(out=st_sq_bb[:], in0=st_sq[:], in1=b_sq[:], op=ALU.mult)
-        one_plus = keep.tile([P, 1], F32)
-        nc.gpsimd.tensor_scalar(out=one_plus[:], in0=st_sq_bb[:], scalar1=1.0, scalar2=None, op0=ALU.add)
+        two_st = keep.tile([P, 1], F32)
+        half_st = keep.tile([P, 1], F32)
+        neg_half_ct = keep.tile([P, 1], F32)
+        neg_st = keep.tile([P, 1], F32)
+        neg_ct_sq = keep.tile([P, 1], F32)
+        four_st_sq_bb = keep.tile([P, 1], F32)
+        delta = keep.tile([P, 1], F32)
         b_term = keep.tile([P, N], F32)
-        nc.vector.tensor_scalar(out=b_term[:], in0=b_rows[:], scalar1=st[:, 0:1], scalar2=None, op0=ALU.mult)
 
-        for grp in range(GROUPS):
-            h_sq_parts = small.tile([P, GROUP, HALVES], F32)
-            h_b_parts = small.tile([P, GROUP, HALVES], F32)
-            for j in range(GROUP):
-                i = grp * GROUP + j
-                sp = x_all[:, i, 0:K]
-                sq_junk = work.tile([P, K], BF16)
-                sp_sq = small.tile([P, 1], F32)
-                nc.scalar.activation(out=sq_junk[:], in_=sp, func=ACT.Square, accum_out=sp_sq[:])
-                sp_sq_min = small.tile([P, 1], F32)
-                nc.gpsimd.tensor_scalar(out=sp_sq_min[:], in0=sp_sq[:], scalar1=MIN_SQ, scalar2=None, op0=ALU.max)
-                inv_norm = small.tile([P, 1], F32)
-                nc.gpsimd.tensor_tensor(out=inv_norm[:], in0=sp_sq_min[:], in1=neg_half[:, 0:1], op=ALU.pow)
-                row_scale = small.tile([P, 1], F32)
-                nc.gpsimd.tensor_tensor(out=row_scale[:], in0=dist[:, i : i + 1], in1=inv_norm[:], op=ALU.mult)
-                u_bf = work.tile([P, K], BF16, align_bytes=64)
-                nc.vector.tensor_scalar(out=u_bf[:], in0=sp, scalar1=row_scale[:, 0:1], scalar2=None, op0=ALU.mult)
-
-                turned = turn.tile([P, PASSES, 2, P], F32)
-                u_words = u_bf[:].bitcast(F32)
-                for g in range(PASSES):
-                    for w in range(2):
-                        nc.tensor.transpose(turned[:, g, w, :], u_words[:, 256 * g + w : 256 * (g + 1) : 2], ident[:])
-                grouped = work.tile([P, PASSES * P * 4], BF16, align_bytes=64)
-                nc.scalar.copy(
-                    out=grouped[:].bitcast(F32).rearrange("p (g r w) -> p g r w", g=PASSES, w=2),
-                    in_=turned[:].rearrange("p g w r -> p g r w"),
-                )
-                nc.vector.quantize_mx(out=u_codes[:, i, :].bitcast(FP8X4), scales=u_scales[:, i, :], in_=grouped[:])
-
-                for nh in range(HALVES):
-                    h_bank = sums.tile([P, BANK], F32)
-                    multiply(nc, h_bank, u_codes, u_scales, w_codes, w_scales, i, nh)
-                    hh_junk = work.tile([P, BANK], BF16)
-                    nc.scalar.activation(
-                        out=hh_junk[:], in_=h_bank[:], func=ACT.Square, accum_out=h_sq_parts[:, j, nh : nh + 1]
-                    )
-                    hb_junk = work.tile([P, BANK], F32)
-                    nc.vector.scalar_tensor_tensor(
-                        out=hb_junk[:], in0=h_bank[:], scalar=1.0, in1=b_rows[:, nh * BANK : (nh + 1) * BANK],
-                        op0=ALU.mult, op1=ALU.mult, accum_out=h_b_parts[:, j, nh : nh + 1],
-                    )
-
-            h_sq = small.tile([P, GROUP], F32)
-            nc.vector.scalar_tensor_tensor(
-                out=h_sq[:], in0=h_sq_parts[:, :, 0], scalar=MIN_SQ, in1=h_sq_parts[:, :, 1], op0=ALU.max, op1=ALU.add
+        def bias_scalars():
+            nc.vector.tensor_scalar(
+                out=half_ct[:], in0=t_exp[:], scalar1=t_exp_neg[:, 0:1], scalar2=0.25, op0=ALU.add, op1=ALU.mult
             )
-            h_b = small.tile([P, GROUP], F32)
-            nc.vector.tensor_tensor(out=h_b[:], in0=h_b_parts[:, :, 0], in1=h_b_parts[:, :, 1], op=ALU.add)
-            r_inv = small.tile([P, GROUP], F32)
-            nc.gpsimd.tensor_tensor(out=r_inv[:], in0=h_sq[:], in1=neg_half[:], op=ALU.pow)
-            r_len = small.tile([P, GROUP], F32)
-            nc.gpsimd.tensor_tensor(out=r_len[:], in0=h_sq[:], in1=r_inv[:], op=ALU.mult)
-            r_arg = small.tile([P, GROUP], F32)
-            nc.gpsimd.tensor_scalar(out=r_arg[:], in0=r_len[:], scalar1=MAX_ARG, scalar2=None, op0=ALU.min)
-            r_exp = small.tile([P, GROUP], F32)
-            nc.scalar.activation(out=r_exp[:], in_=r_arg[:], func=ACT.Exp)
-            r_exp_neg = small.tile([P, GROUP], F32)
-            nc.scalar.activation(out=r_exp_neg[:], in_=r_arg[:], func=ACT.Exp, scale=-1.0)
-            r_tanh = small.tile([P, GROUP], F32)
-            nc.scalar.activation(out=r_tanh[:], in_=r_arg[:], func=ACT.Tanh, scale=0.5)
-            along = small.tile([P, GROUP], F32)
-            nc.gpsimd.tensor_tensor(out=along[:], in0=h_b[:], in1=r_inv[:], op=ALU.mult)
-            two_sinh = small.tile([P, GROUP], F32)
-            nc.gpsimd.tensor_tensor(out=two_sinh[:], in0=r_exp[:], in1=r_exp_neg[:], op=ALU.subtract)
-            two_c1 = small.tile([P, GROUP], F32)
-            nc.gpsimd.tensor_tensor(out=two_c1[:], in0=two_sinh[:], in1=r_inv[:], op=ALU.mult)
-            lift = small.tile([P, GROUP], F32)
-            nc.gpsimd.tensor_tensor(out=lift[:], in0=r_tanh[:], in1=along[:], op=ALU.mult)
-            mix = small.tile([P, GROUP], F32)
-            nc.gpsimd.tensor_scalar(
-                out=mix[:], in0=lift[:], scalar1=half_st[:, 0:1], scalar2=half_ct[:, 0:1], op0=ALU.mult, op1=ALU.add
+            nc.vector.tensor_scalar(
+                out=two_st[:], in0=t_exp[:], scalar1=t_exp_neg[:, 0:1], scalar2=t_inv[:, 0:1],
+                op0=ALU.subtract, op1=ALU.mult,
             )
-            coef = small.tile([P, GROUP], F32)
-            nc.gpsimd.tensor_tensor(out=coef[:], in0=two_c1[:], in1=mix[:], op=ALU.mult)
+            nc.vector.tensor_scalar(out=half_st[:], in0=two_st[:], scalar1=0.25, scalar2=None, op0=ALU.mult)
+            nc.vector.tensor_scalar(out=neg_st[:], in0=two_st[:], scalar1=-0.5, scalar2=None, op0=ALU.mult)
+            nc.vector.tensor_scalar(out=neg_half_ct[:], in0=half_ct[:], scalar1=-1.0, scalar2=None, op0=ALU.mult)
+            nc.vector.tensor_scalar(
+                out=neg_ct_sq[:], in0=half_ct[:], scalar1=half_ct[:, 0:1], scalar2=-4.0, op0=ALU.mult, op1=ALU.mult
+            )
+            nc.vector.tensor_scalar(
+                out=four_st_sq_bb[:], in0=two_st[:], scalar1=two_st[:, 0:1], scalar2=b_sq[:, 0:1],
+                op0=ALU.mult, op1=ALU.mult,
+            )
+            nc.vector.tensor_scalar(
+                out=delta[:], in0=four_st_sq_bb[:], scalar1=0.25, scalar2=neg_ct_sq[:, 0:1], op0=ALU.mult, op1=ALU.add
+            )
+            nc.vector.tensor_scalar(
+                out=b_term[:], in0=b_rows[:], scalar1=two_st[:, 0:1], scalar2=0.5, op0=ALU.mult, op1=ALU.mult
+            )
 
-            cross = small.tile([P, GROUP], F32)
-            nc.gpsimd.tensor_scalar(out=cross[:], in0=h_b[:], scalar1=two_st[:, 0:1], scalar2=None, op0=ALU.mult)
-            o_sq_a = small.tile([P, GROUP], F32)
-            nc.gpsimd.tensor_tensor(out=o_sq_a[:], in0=coef[:], in1=h_sq[:], op=ALU.mult)
-            o_sq_b = small.tile([P, GROUP], F32)
-            nc.gpsimd.tensor_tensor(out=o_sq_b[:], in0=o_sq_a[:], in1=cross[:], op=ALU.add)
-            o_sq_c = small.tile([P, GROUP], F32)
-            nc.gpsimd.tensor_tensor(out=o_sq_c[:], in0=o_sq_b[:], in1=coef[:], op=ALU.mult)
-            time_sq = small.tile([P, GROUP], F32)
-            nc.gpsimd.tensor_scalar(out=time_sq[:], in0=o_sq_c[:], scalar1=one_plus[:, 0:1], scalar2=None, op0=ALU.add)
-            time_co = small.tile([P, GROUP], F32)
-            nc.gpsimd.tensor_tensor(out=time_co[:], in0=time_sq[:], in1=half[:, 0:GROUP], op=ALU.pow)
+        def squares_of_period(q):
+            if q == -2:
+                return [3]
+            if q in (0, 1):
+                return [4 + 2 * q, 5 + 2 * q]
+            if q >= 2 and q + 6 < TILES:
+                return [q + 6]
+            return []
 
-            o_grp = work.tile([P, GROUP, N + 1], F32)
-            nc.vector.tensor_copy(out=o_grp[:, :, 0], in_=time_co[:])
-            for j in range(GROUP):
-                i = grp * GROUP + j
-                for nh in range(HALVES):
-                    o_bank = sums.tile([P, BANK], F32)
-                    multiply(nc, o_bank, u_codes, u_scales, w_codes, w_scales, i, nh)
-                    nc.vector.scalar_tensor_tensor(
-                        out=o_grp[:, j, 1 + nh * BANK : 1 + (nh + 1) * BANK],
-                        in0=o_bank[:],
-                        scalar=coef[:, j : j + 1],
-                        in1=b_term[:, nh * BANK : (nh + 1) * BANK],
-                        op0=ALU.mult,
-                        op1=ALU.add,
-                    )
-                nc.sync.dma_start(out=out[i * P : (i + 1) * P, :], in_=o_grp[:, j, :])
+        def time_group_ending_at(i):
+            if i < 0 or i >= TILES:
+                return None
+            if i >= TILES - 2:
+                return (i, 1)
+            if i % 2 == 1:
+                return (i - 1, 2)
+            return None
+
+        for q in range(-2, TILES + 2):
+            if 0 <= q + 2 < TILES:
+                turn_rows(q + 2)
+            if 0 <= q < TILES:
+                sum_h_bias(q, 0)
+                sum_h_squared(q, 1)
+            if 0 <= q - 1 < TILES:
+                exponentials(q - 1)
+            if 0 <= q < TILES:
+                sum_h_bias(q, 1)
+                sum_h_squared(q, 0)
+            if 0 <= q - 1 < TILES:
+                chain_y(q - 1)
+            if 0 <= q + 2 < TILES:
+                regroup(q + 2)
+            if 0 <= q - 1 < TILES:
+                chain_x(q - 1)
+            group = time_group_ending_at(q - 2)
+            if group is not None:
+                place_times(group[0], group[1])
+            if 0 <= q - 2 < TILES:
+                finish(q - 2, 0)
+            if 0 <= q < TILES:
+                chain_h_sq(q)
+                chain_r_inv(q)
+            if 0 <= q - 2 < TILES:
+                finish(q - 2, 1)
+            if group is not None:
+                for i in range(group[0], group[0] + group[1]):
+                    store(i)
+            if 0 <= q + 1 < TILES:
+                multiply(q + 1)
+            for i in squares_of_period(q):
+                square_rows(i)
+                if i % 2 == 1:
+                    inverse_norms(i - 1, 2)
+            if 0 <= q - 1 < TILES:
+                chain_coef(q - 1)
+            group = time_group_ending_at(q - 1)
+            if group is not None:
+                time_coordinates(group[0], group[1])
+            if 0 <= q + 2 < TILES:
+                quantise(q + 2)
+            if q == -2:
+                bias_scalars()
+            if 2 <= q + 3 < TILES:
+                scale_rows(q + 3)
+            if 0 <= q < TILES:
+                chain_after_r_inv(q)

@@ -22,6 +22,8 @@ BANK = 512
 HALVES = N // BANK
 TILES = ROWS // P
 O_PITCH = 1032
+X_PITCH = 1040
+WHOLE = 2
 
 EPS = 1e-7
 MIN_SQ = 1e-30
@@ -54,20 +56,29 @@ def tile_hyperboliclinearhyperboloid_kernel(tc, x, weight_words, weight_scales, 
         ident = keep.tile([P, P], F32)
         make_identity(nc, ident[:])
 
-        x_all = keep.tile([P, TILES, K], BF16)
+        x_all = keep.tile([P, TILES, X_PITCH], BF16)
         x_time = keep.tile([P, TILES], BF16)
         b_rows = keep.tile([P, N], BF16)
 
-        def load_rows(i):
-            nc.sync.dma_start(out=x_all[:, i, :], in_=x[i * P : (i + 1) * P, 1 : K + 1])
+        def spatial(i):
+            if i < WHOLE:
+                return x_all[:, i, 1 : K + 1]
+            return x_all[:, i, 0:K]
 
+        def load_rows(i):
+            if i < WHOLE:
+                nc.sync.dma_start(out=x_all[:, i, 0 : K + 1], in_=x[i * P : (i + 1) * P, :])
+            else:
+                nc.sync.dma_start(out=x_all[:, i, 0:K], in_=x[i * P : (i + 1) * P, 1 : K + 1])
+
+        for i in range(WHOLE):
+            load_rows(i)
         with nc.allow_non_contiguous_dma(reason="one bfloat16 element of each row of x"):
-            nc.sync.dma_start(out=x_time[:], in_=x[:, 0:1].rearrange("(i p) o -> p (i o)", p=P))
-        load_rows(0)
-        load_rows(1)
+            nc.sync.dma_start(
+                out=x_time[:, WHOLE:TILES], in_=x[WHOLE * P : ROWS, 0:1].rearrange("(i p) o -> p (i o)", p=P)
+            )
         nc.sync.dma_start(out=b_rows[:], in_=bias.rearrange("o n -> (o n)").partition_broadcast(P))
-        load_rows(2)
-        load_rows(3)
+        load_rows(WHOLE)
         for g in range(PASSES):
             nc.sync.dma_start(
                 out=w_codes[:, g, :].bitcast(I32),
@@ -79,7 +90,7 @@ def tile_hyperboliclinearhyperboloid_kernel(tc, x, weight_words, weight_scales, 
                     out=w_scales[32 * quad : 32 * quad + 4, g, :].bitcast(I32),
                     in_=weight_scales[g, 4 * quad : 4 * quad + 4, :].bitcast(I32),
                 )
-        for i in range(4, TILES):
+        for i in range(WHOLE + 1, TILES):
             load_rows(i)
 
         u_codes = keep.tile([P, TILES, PASSES * P], U32, align_bytes=64)
@@ -113,8 +124,8 @@ def tile_hyperboliclinearhyperboloid_kernel(tc, x, weight_words, weight_scales, 
         bank_of = {}
 
         def square_rows(i):
-            sp = x_all[:, i, :]
-            if i % 2 == 1 and i < 8:
+            sp = spatial(i)
+            if i in (1, 3, 5):
                 sq_v = junk.tile([P, K], F32)
                 nc.vector.scalar_tensor_tensor(
                     out=sq_v[:], in0=sp, scalar=1.0, in1=sp, op0=ALU.mult, op1=ALU.mult, accum_out=col(sp_sq, i)
@@ -131,7 +142,7 @@ def tile_hyperboliclinearhyperboloid_kernel(tc, x, weight_words, weight_scales, 
         def scale_rows(i):
             u_bf = work.tile([P, K], BF16, align_bytes=64)
             nc.vector.tensor_scalar(
-                out=u_bf[:], in0=x_all[:, i, :], scalar1=col(inv_norm, i), scalar2=col(dist, i), op0=ALU.mult, op1=ALU.mult
+                out=u_bf[:], in0=spatial(i), scalar1=col(inv_norm, i), scalar2=col(dist, i), op0=ALU.mult, op1=ALU.mult
             )
             u_of[i] = u_bf
 
@@ -185,7 +196,7 @@ def tile_hyperboliclinearhyperboloid_kernel(tc, x, weight_words, weight_scales, 
             )
 
         def chain_h_sq(i):
-            nc.vector.tensor_scalar(
+            nc.gpsimd.tensor_scalar(
                 out=col(h_sq, i), in0=h_sq_parts[:, i, 0:1], scalar1=h_sq_parts[:, i, 1:2], scalar2=MIN_SQ,
                 op0=ALU.add, op1=ALU.max,
             )
@@ -194,26 +205,26 @@ def tile_hyperboliclinearhyperboloid_kernel(tc, x, weight_words, weight_scales, 
             nc.gpsimd.tensor_tensor(out=col(r_inv, i), in0=col(h_sq, i), in1=neg_half[:, 0:1], op=ALU.pow)
 
         def chain_after_r_inv(i):
-            nc.vector.tensor_scalar(
+            nc.gpsimd.tensor_scalar(
                 out=col(r_arg, i), in0=col(h_sq, i), scalar1=col(r_inv, i), scalar2=MAX_ARG, op0=ALU.mult, op1=ALU.min
             )
-            nc.vector.tensor_scalar(
+            nc.gpsimd.tensor_scalar(
                 out=col(along, i), in0=h_b_parts[:, i, 0:1], scalar1=h_b_parts[:, i, 1:2], scalar2=col(r_inv, i),
                 op0=ALU.add, op1=ALU.mult,
-            )
-            nc.vector.tensor_scalar(
-                out=col(shift, i), in0=col(along, i), scalar1=col(r_inv, i), scalar2=neg_st[:, 0:1],
-                op0=ALU.mult, op1=ALU.mult,
             )
 
         def exponentials(i):
             nc.scalar.activation(out=col(r_exp, i), in_=col(r_arg, i), func=ACT.Exp)
             nc.scalar.activation(out=col(r_exp_neg, i), in_=col(r_arg, i), func=ACT.Exp, scale=-1.0)
-            nc.scalar.activation(
-                out=col(y_fac, i), in_=col(along, i), func=ACT.Identity, scale=half_st[:, 0:1], bias=neg_half_ct[:, 0:1]
+
+        def chain_factors(i):
+            nc.gpsimd.tensor_scalar(
+                out=col(y_fac, i), in0=col(along, i), scalar1=half_st[:, 0:1], scalar2=half_ct[:, 0:1],
+                op0=ALU.mult, op1=ALU.subtract,
             )
-            nc.scalar.activation(
-                out=col(x_fac, i), in_=col(along, i), func=ACT.Identity, scale=half_st[:, 0:1], bias=half_ct[:, 0:1]
+            nc.gpsimd.tensor_scalar(
+                out=col(x_fac, i), in0=col(along, i), scalar1=half_st[:, 0:1], scalar2=half_ct[:, 0:1],
+                op0=ALU.mult, op1=ALU.add,
             )
 
         def chain_y(i):
@@ -224,10 +235,13 @@ def tile_hyperboliclinearhyperboloid_kernel(tc, x, weight_words, weight_scales, 
                 out=col(x_less_y, i), in_=col(r_exp, i), func=ACT.Identity, scale=col(x_fac, i), bias=col(y_neg, i)
             )
 
-        def chain_coef(i):
+        def chain_shift(i):
             nc.scalar.activation(
-                out=col(coef, i), in_=col(x_less_y, i), func=ACT.Identity, scale=col(r_inv, i), bias=col(shift, i)
+                out=col(shift, i), in_=col(along, i), func=ACT.Identity, scale=neg_st[:, 0:1], bias=col(x_less_y, i)
             )
+
+        def chain_coef(i):
+            nc.scalar.activation(out=col(coef, i), in_=col(shift, i), func=ACT.Identity, scale=col(r_inv, i))
             nc.scalar.activation(
                 out=col(z_sq, i), in_=col(y_neg, i), func=ACT.Square, scale=-2.0, bias=col(x_less_y, i)
             )
@@ -240,7 +254,7 @@ def tile_hyperboliclinearhyperboloid_kernel(tc, x, weight_words, weight_scales, 
             nc.gpsimd.tensor_tensor(out=time_co[:, cols], in0=time_sq[:, cols], in1=half[:, 0:n], op=ALU.pow)
 
         def place_times(i, n):
-            nc.vector.tensor_copy(out=o_all[:, i : i + n, 0], in_=time_co[:, i : i + n])
+            nc.scalar.copy(out=o_all[:, i : i + n, 0], in_=time_co[:, i : i + n])
 
         def finish(i, nh):
             nc.vector.scalar_tensor_tensor(
@@ -255,51 +269,40 @@ def tile_hyperboliclinearhyperboloid_kernel(tc, x, weight_words, weight_scales, 
         def store(i):
             nc.sync.dma_start(out=out[i * P : (i + 1) * P, :], in_=o_all[:, i, 0 : N + 1])
 
-        warm = keep.tile([P, 2], F32)
-        nc.scalar.activation(out=warm[:, 0:1], in_=half[:, 0:1], func=ACT.Ln)
         theta = keep.tile([P, TILES], F32)
-        nc.vector.tensor_scalar(out=theta[:], in0=x_time[:], scalar1=1.0 + EPS, scalar2=None, op0=ALU.max)
         theta_less = keep.tile([P, TILES], F32)
-        nc.vector.tensor_scalar(out=theta_less[:], in0=theta[:], scalar1=-1.0, scalar2=None, op0=ALU.add)
         below = keep.tile([P, TILES], F32)
-        nc.vector.scalar_tensor_tensor(
-            out=below[:], in0=theta[:], scalar=1.0, in1=theta_less[:], op0=ALU.add, op1=ALU.mult
-        )
         root = keep.tile([P, TILES], F32)
-        nc.gpsimd.tensor_tensor(out=root[:], in0=below[:], in1=half[:], op=ALU.pow)
         ln_arg = keep.tile([P, TILES], F32)
-        nc.vector.tensor_tensor(out=ln_arg[:], in0=theta[:], in1=root[:], op=ALU.add)
-        square_rows(0)
-        square_rows(1)
         dist = keep.tile([P, TILES], F32)
-        nc.scalar.activation(out=dist[:], in_=ln_arg[:], func=ACT.Ln)
-        nc.scalar.activation(out=warm[:, 1:2], in_=half[:, 0:1], func=ACT.Exp)
-        square_rows(2)
-        inverse_norms(0, 2)
 
-        b_junk = junk.tile([P, N], F32)
+        def distance_start(a, b, times):
+            nc.vector.tensor_scalar(out=theta[:, a:b], in0=times, scalar1=1.0 + EPS, scalar2=None, op0=ALU.max)
+            nc.vector.tensor_scalar(out=theta_less[:, a:b], in0=theta[:, a:b], scalar1=-1.0, scalar2=None, op0=ALU.add)
+            nc.vector.scalar_tensor_tensor(
+                out=below[:, a:b], in0=theta[:, a:b], scalar=1.0, in1=theta_less[:, a:b], op0=ALU.add, op1=ALU.mult
+            )
+
+        def distance_root(a, b):
+            nc.gpsimd.tensor_tensor(out=root[:, a:b], in0=below[:, a:b], in1=half[:, a:b], op=ALU.pow)
+
+        def distance_sum(a, b):
+            nc.vector.tensor_tensor(out=ln_arg[:, a:b], in0=theta[:, a:b], in1=root[:, a:b], op=ALU.add)
+
+        def distance_end(a, b):
+            nc.scalar.activation(out=dist[:, a:b], in_=ln_arg[:, a:b], func=ACT.Ln)
+
         b_sq = keep.tile([P, 1], F32)
-        nc.vector.scalar_tensor_tensor(
-            out=b_junk[:], in0=b_rows[:], scalar=1.0, in1=b_rows[:], op0=ALU.mult, op1=ALU.mult, accum_out=b_sq[:]
-        )
         b_sq_min = keep.tile([P, 1], F32)
-        nc.vector.tensor_scalar(out=b_sq_min[:], in0=b_sq[:], scalar1=1e-15, scalar2=None, op0=ALU.max)
         t_raw = keep.tile([P, 1], F32)
-        nc.gpsimd.tensor_tensor(out=t_raw[:], in0=b_sq_min[:], in1=half[:, 0:1], op=ALU.pow)
-        scale_rows(0)
-        scale_rows(1)
         t_arg = keep.tile([P, 1], F32)
-        nc.vector.tensor_scalar(out=t_arg[:], in0=t_raw[:], scalar1=1e-15, scalar2=MAX_ARG, op0=ALU.max, op1=ALU.min)
         t_inv = keep.tile([P, 1], F32)
-        nc.vector.reciprocal(out=t_inv[:], in_=t_arg[:])
         t_exp = keep.tile([P, 1], F32)
-        nc.scalar.activation(out=t_exp[:], in_=t_arg[:], func=ACT.Exp)
         t_exp_neg = keep.tile([P, 1], F32)
-        nc.scalar.activation(out=t_exp_neg[:], in_=t_arg[:], func=ACT.Exp, scale=-1.0)
         half_ct = keep.tile([P, 1], F32)
+        neg_half_ct = keep.tile([P, 1], F32)
         two_st = keep.tile([P, 1], F32)
         half_st = keep.tile([P, 1], F32)
-        neg_half_ct = keep.tile([P, 1], F32)
         neg_st = keep.tile([P, 1], F32)
         neg_ct_sq = keep.tile([P, 1], F32)
         four_st_sq_bb = keep.tile([P, 1], F32)
@@ -314,9 +317,11 @@ def tile_hyperboliclinearhyperboloid_kernel(tc, x, weight_words, weight_scales, 
                 out=two_st[:], in0=t_exp[:], scalar1=t_exp_neg[:, 0:1], scalar2=t_inv[:, 0:1],
                 op0=ALU.subtract, op1=ALU.mult,
             )
+            nc.vector.tensor_scalar(out=neg_half_ct[:], in0=half_ct[:], scalar1=-1.0, scalar2=None, op0=ALU.mult)
             nc.vector.tensor_scalar(out=half_st[:], in0=two_st[:], scalar1=0.25, scalar2=None, op0=ALU.mult)
             nc.vector.tensor_scalar(out=neg_st[:], in0=two_st[:], scalar1=-0.5, scalar2=None, op0=ALU.mult)
-            nc.vector.tensor_scalar(out=neg_half_ct[:], in0=half_ct[:], scalar1=-1.0, scalar2=None, op0=ALU.mult)
+
+        def bias_terms():
             nc.vector.tensor_scalar(
                 out=neg_ct_sq[:], in0=half_ct[:], scalar1=half_ct[:, 0:1], scalar2=-4.0, op0=ALU.mult, op1=ALU.mult
             )
@@ -331,13 +336,61 @@ def tile_hyperboliclinearhyperboloid_kernel(tc, x, weight_words, weight_scales, 
                 out=b_term[:], in0=b_rows[:], scalar1=two_st[:, 0:1], scalar2=0.5, op0=ALU.mult, op1=ALU.mult
             )
 
+        warm = keep.tile([P, 1], F32)
+        nc.scalar.activation(out=warm[:], in_=half[:, 0:1], func=ACT.Ln)
+        square_rows(0)
+        distance_start(0, WHOLE, x_all[:, 0:WHOLE, 0])
+        distance_root(0, WHOLE)
+        inverse_norms(0, 1)
+        square_rows(1)
+        inverse_norms(1, 1)
+        distance_sum(0, WHOLE)
+        distance_end(0, WHOLE)
+        scale_rows(0)
+        turn_rows(0)
+        distance_start(WHOLE, TILES, x_time[:, WHOLE:TILES])
+        scale_rows(1)
+        turn_rows(1)
+        b_junk = junk.tile([P, N], F32)
+        nc.vector.scalar_tensor_tensor(
+            out=b_junk[:], in0=b_rows[:], scalar=1.0, in1=b_rows[:], op0=ALU.mult, op1=ALU.mult, accum_out=b_sq[:]
+        )
+        nc.vector.tensor_scalar(out=b_sq_min[:], in0=b_sq[:], scalar1=1e-15, scalar2=None, op0=ALU.max)
+        distance_root(WHOLE, TILES)
+        nc.gpsimd.tensor_tensor(out=t_raw[:], in0=b_sq_min[:], in1=half[:, 0:1], op=ALU.pow)
+        square_rows(2)
+        inverse_norms(2, 1)
+        regroup(0)
+        quantise(0)
+        multiply(0)
+        regroup(1)
+        quantise(1)
+
+        def fronts_of_period(q):
+            if q == 1:
+                return [2]
+            if q == 2:
+                return [3, 4]
+            if q >= 3 and q + 2 < TILES:
+                return [q + 2]
+            return []
+
+        def scalings_of_period(q):
+            if q == 0:
+                return [2]
+            if q == 1:
+                return [3, 4]
+            if q >= 2 and q + 3 < TILES:
+                return [q + 3]
+            return []
+
         def squares_of_period(q):
-            if q == -2:
-                return [3]
-            if q in (0, 1):
-                return [4 + 2 * q, 5 + 2 * q]
-            if q >= 2 and q + 6 < TILES:
-                return [q + 6]
+            if q == 0:
+                return [3, 4]
+            if q == 1:
+                return [5, 6]
+            if q >= 2 and q + 5 < TILES:
+                return [q + 5]
             return []
 
         def time_group_ending_at(i):
@@ -349,52 +402,72 @@ def tile_hyperboliclinearhyperboloid_kernel(tc, x, weight_words, weight_scales, 
                 return (i - 1, 2)
             return None
 
-        for q in range(-2, TILES + 2):
-            if 0 <= q + 2 < TILES:
-                turn_rows(q + 2)
-            if 0 <= q < TILES:
+        for q in range(0, TILES + 2):
+            for i in fronts_of_period(q):
+                turn_rows(i)
+            if 0 <= q - 1 < TILES:
+                chain_factors(q - 1)
+            if q < TILES:
                 sum_h_bias(q, 0)
+            if q < TILES:
                 sum_h_squared(q, 1)
-            if 0 <= q - 1 < TILES:
-                exponentials(q - 1)
-            if 0 <= q < TILES:
-                sum_h_bias(q, 1)
-                sum_h_squared(q, 0)
-            if 0 <= q - 1 < TILES:
-                chain_y(q - 1)
-            if 0 <= q + 2 < TILES:
-                regroup(q + 2)
-            if 0 <= q - 1 < TILES:
-                chain_x(q - 1)
+            if 0 <= q - 2 < TILES:
+                chain_coef(q - 2)
             group = time_group_ending_at(q - 2)
             if group is not None:
-                place_times(group[0], group[1])
-            if 0 <= q - 2 < TILES:
-                finish(q - 2, 0)
-            if 0 <= q < TILES:
+                time_coordinates(group[0], group[1])
+            if 0 <= q - 1 < TILES:
+                exponentials(q - 1)
+            if q < TILES:
+                sum_h_bias(q, 1)
+            if q < TILES:
+                sum_h_squared(q, 0)
+            if q == 0:
+                distance_sum(WHOLE, TILES)
+                distance_end(WHOLE, TILES)
+                nc.vector.tensor_scalar(
+                    out=t_arg[:], in0=t_raw[:], scalar1=1e-15, scalar2=MAX_ARG, op0=ALU.max, op1=ALU.min
+                )
+                nc.vector.reciprocal(out=t_inv[:], in_=t_arg[:])
+            if q == 0:
+                nc.scalar.activation(out=t_exp[:], in_=t_arg[:], func=ACT.Exp)
+                nc.scalar.activation(out=t_exp_neg[:], in_=t_arg[:], func=ACT.Exp, scale=-1.0)
+            if q < TILES:
                 chain_h_sq(q)
                 chain_r_inv(q)
+                chain_after_r_inv(q)
+            if 0 <= q - 1 < TILES:
+                chain_y(q - 1)
+            for i in fronts_of_period(q):
+                regroup(i)
+            if 0 <= q - 1 < TILES:
+                chain_x(q - 1)
+            if 0 <= q - 2 < TILES:
+                finish(q - 2, 0)
             if 0 <= q - 2 < TILES:
                 finish(q - 2, 1)
-            if group is not None:
-                for i in range(group[0], group[0] + group[1]):
-                    store(i)
-            if 0 <= q + 1 < TILES:
+            for i in fronts_of_period(q):
+                quantise(i)
+            if q + 1 < TILES:
                 multiply(q + 1)
             for i in squares_of_period(q):
                 square_rows(i)
-                if i % 2 == 1:
+                if i < 6:
+                    inverse_norms(i, 1)
+                elif i % 2 == 1:
                     inverse_norms(i - 1, 2)
             if 0 <= q - 1 < TILES:
-                chain_coef(q - 1)
-            group = time_group_ending_at(q - 1)
+                chain_shift(q - 1)
+            group = time_group_ending_at(q - 2)
             if group is not None:
-                time_coordinates(group[0], group[1])
-            if 0 <= q + 2 < TILES:
-                quantise(q + 2)
-            if q == -2:
+                place_times(group[0], group[1])
+            group = time_group_ending_at(q - 2)
+            if group is not None:
+                for i in range(group[0], group[0] + group[1]):
+                    store(i)
+            for i in scalings_of_period(q):
+                scale_rows(i)
+            if q == 0:
                 bias_scalars()
-            if 2 <= q + 3 < TILES:
-                scale_rows(q + 3)
-            if 0 <= q < TILES:
-                chain_after_r_inv(q)
+            if q == 0:
+                bias_terms()

@@ -125,7 +125,7 @@ def tile_hyperboliclinearhyperboloid_kernel(tc, x, weight_words, weight_scales, 
 
         def square_rows(i):
             sp = spatial(i)
-            if i in (1, 3, 5):
+            if i in (1, 4, 6):
                 sq_v = junk.tile([P, K], F32)
                 nc.vector.scalar_tensor_tensor(
                     out=sq_v[:], in0=sp, scalar=1.0, in1=sp, op0=ALU.mult, op1=ALU.mult, accum_out=col(sp_sq, i)
@@ -196,7 +196,7 @@ def tile_hyperboliclinearhyperboloid_kernel(tc, x, weight_words, weight_scales, 
             )
 
         def chain_h_sq(i):
-            nc.gpsimd.tensor_scalar(
+            nc.vector.tensor_scalar(
                 out=col(h_sq, i), in0=h_sq_parts[:, i, 0:1], scalar1=h_sq_parts[:, i, 1:2], scalar2=MIN_SQ,
                 op0=ALU.add, op1=ALU.max,
             )
@@ -205,10 +205,10 @@ def tile_hyperboliclinearhyperboloid_kernel(tc, x, weight_words, weight_scales, 
             nc.gpsimd.tensor_tensor(out=col(r_inv, i), in0=col(h_sq, i), in1=neg_half[:, 0:1], op=ALU.pow)
 
         def chain_after_r_inv(i):
-            nc.gpsimd.tensor_scalar(
+            nc.vector.tensor_scalar(
                 out=col(r_arg, i), in0=col(h_sq, i), scalar1=col(r_inv, i), scalar2=MAX_ARG, op0=ALU.mult, op1=ALU.min
             )
-            nc.gpsimd.tensor_scalar(
+            nc.vector.tensor_scalar(
                 out=col(along, i), in0=h_b_parts[:, i, 0:1], scalar1=h_b_parts[:, i, 1:2], scalar2=col(r_inv, i),
                 op0=ALU.add, op1=ALU.mult,
             )
@@ -216,32 +216,32 @@ def tile_hyperboliclinearhyperboloid_kernel(tc, x, weight_words, weight_scales, 
         def exponentials(i):
             nc.scalar.activation(out=col(r_exp, i), in_=col(r_arg, i), func=ACT.Exp)
             nc.scalar.activation(out=col(r_exp_neg, i), in_=col(r_arg, i), func=ACT.Exp, scale=-1.0)
-
-        def chain_factors(i):
-            nc.gpsimd.tensor_scalar(
-                out=col(y_fac, i), in0=col(along, i), scalar1=half_st[:, 0:1], scalar2=half_ct[:, 0:1],
-                op0=ALU.mult, op1=ALU.subtract,
+            nc.scalar.activation(
+                out=col(y_fac, i), in_=col(along, i), func=ACT.Identity, scale=half_st[:, 0:1], bias=neg_half_ct[:, 0:1]
             )
-            nc.gpsimd.tensor_scalar(
-                out=col(x_fac, i), in0=col(along, i), scalar1=half_st[:, 0:1], scalar2=half_ct[:, 0:1],
+            nc.scalar.activation(
+                out=col(x_fac, i), in_=col(along, i), func=ACT.Identity, scale=half_st[:, 0:1], bias=half_ct[:, 0:1]
+            )
+            nc.scalar.activation(out=col(shift, i), in_=col(along, i), func=ACT.Identity, scale=st[:, 0:1])
+
+        def chain_y(i):
+            nc.vector.tensor_scalar(
+                out=col(y_neg, i), in0=col(r_exp_neg, i), scalar1=col(y_fac, i), scalar2=None, op0=ALU.mult
+            )
+
+        def chain_x(i):
+            nc.vector.tensor_scalar(
+                out=col(x_less_y, i), in0=col(r_exp, i), scalar1=col(x_fac, i), scalar2=col(y_neg, i),
                 op0=ALU.mult, op1=ALU.add,
             )
 
-        def chain_y(i):
-            nc.scalar.activation(out=col(y_neg, i), in_=col(r_exp_neg, i), func=ACT.Identity, scale=col(y_fac, i))
-
-        def chain_x(i):
-            nc.scalar.activation(
-                out=col(x_less_y, i), in_=col(r_exp, i), func=ACT.Identity, scale=col(x_fac, i), bias=col(y_neg, i)
-            )
-
-        def chain_shift(i):
-            nc.scalar.activation(
-                out=col(shift, i), in_=col(along, i), func=ACT.Identity, scale=neg_st[:, 0:1], bias=col(x_less_y, i)
-            )
-
         def chain_coef(i):
-            nc.scalar.activation(out=col(coef, i), in_=col(shift, i), func=ACT.Identity, scale=col(r_inv, i))
+            nc.vector.tensor_scalar(
+                out=col(coef, i), in0=col(x_less_y, i), scalar1=col(shift, i), scalar2=col(r_inv, i),
+                op0=ALU.subtract, op1=ALU.mult,
+            )
+
+        def chain_z_sq(i):
             nc.scalar.activation(
                 out=col(z_sq, i), in_=col(y_neg, i), func=ACT.Square, scale=-2.0, bias=col(x_less_y, i)
             )
@@ -303,7 +303,7 @@ def tile_hyperboliclinearhyperboloid_kernel(tc, x, weight_words, weight_scales, 
         neg_half_ct = keep.tile([P, 1], F32)
         two_st = keep.tile([P, 1], F32)
         half_st = keep.tile([P, 1], F32)
-        neg_st = keep.tile([P, 1], F32)
+        st = keep.tile([P, 1], F32)
         neg_ct_sq = keep.tile([P, 1], F32)
         four_st_sq_bb = keep.tile([P, 1], F32)
         delta = keep.tile([P, 1], F32)
@@ -319,7 +319,7 @@ def tile_hyperboliclinearhyperboloid_kernel(tc, x, weight_words, weight_scales, 
             )
             nc.vector.tensor_scalar(out=neg_half_ct[:], in0=half_ct[:], scalar1=-1.0, scalar2=None, op0=ALU.mult)
             nc.vector.tensor_scalar(out=half_st[:], in0=two_st[:], scalar1=0.25, scalar2=None, op0=ALU.mult)
-            nc.vector.tensor_scalar(out=neg_st[:], in0=two_st[:], scalar1=-0.5, scalar2=None, op0=ALU.mult)
+            nc.vector.tensor_scalar(out=st[:], in0=two_st[:], scalar1=0.5, scalar2=None, op0=ALU.mult)
 
         def bias_terms():
             nc.vector.tensor_scalar(
@@ -365,24 +365,7 @@ def tile_hyperboliclinearhyperboloid_kernel(tc, x, weight_words, weight_scales, 
         multiply(0)
         regroup(1)
         quantise(1)
-
-        def fronts_of_period(q):
-            if q == 1:
-                return [2]
-            if q == 2:
-                return [3, 4]
-            if q >= 3 and q + 2 < TILES:
-                return [q + 2]
-            return []
-
-        def scalings_of_period(q):
-            if q == 0:
-                return [2]
-            if q == 1:
-                return [3, 4]
-            if q >= 2 and q + 3 < TILES:
-                return [q + 3]
-            return []
+        multiply(1)
 
         def squares_of_period(q):
             if q == 0:
@@ -403,61 +386,75 @@ def tile_hyperboliclinearhyperboloid_kernel(tc, x, weight_words, weight_scales, 
             return None
 
         for q in range(0, TILES + 2):
-            for i in fronts_of_period(q):
-                turn_rows(i)
-            if 0 <= q - 1 < TILES:
-                chain_factors(q - 1)
+            if q >= 1 and q + 3 < TILES:
+                scale_rows(q + 3)
+                turn_rows(q + 3)
             if q < TILES:
                 sum_h_bias(q, 0)
-            if q < TILES:
-                sum_h_squared(q, 1)
-            if 0 <= q - 2 < TILES:
-                chain_coef(q - 2)
-            group = time_group_ending_at(q - 2)
-            if group is not None:
-                time_coordinates(group[0], group[1])
-            if 0 <= q - 1 < TILES:
-                exponentials(q - 1)
-            if q < TILES:
-                sum_h_bias(q, 1)
-            if q < TILES:
-                sum_h_squared(q, 0)
             if q == 0:
                 distance_sum(WHOLE, TILES)
-                distance_end(WHOLE, TILES)
+            if 0 <= q - 2 < TILES:
+                chain_coef(q - 2)
+            if q < TILES:
+                sum_h_bias(q, 1)
+            if 0 <= q - 1 < TILES:
+                chain_after_r_inv(q - 1)
+            if q == 0:
                 nc.vector.tensor_scalar(
                     out=t_arg[:], in0=t_raw[:], scalar1=1e-15, scalar2=MAX_ARG, op0=ALU.max, op1=ALU.min
                 )
                 nc.vector.reciprocal(out=t_inv[:], in_=t_arg[:])
-            if q == 0:
-                nc.scalar.activation(out=t_exp[:], in_=t_arg[:], func=ACT.Exp)
-                nc.scalar.activation(out=t_exp_neg[:], in_=t_arg[:], func=ACT.Exp, scale=-1.0)
-            if q < TILES:
-                chain_h_sq(q)
-                chain_r_inv(q)
-                chain_after_r_inv(q)
-            if 0 <= q - 1 < TILES:
-                chain_y(q - 1)
-            for i in fronts_of_period(q):
-                regroup(i)
-            if 0 <= q - 1 < TILES:
-                chain_x(q - 1)
-            if 0 <= q - 2 < TILES:
-                finish(q - 2, 0)
-            if 0 <= q - 2 < TILES:
-                finish(q - 2, 1)
-            for i in fronts_of_period(q):
-                quantise(i)
-            if q + 1 < TILES:
-                multiply(q + 1)
             for i in squares_of_period(q):
                 square_rows(i)
                 if i < 6:
                     inverse_norms(i, 1)
                 elif i % 2 == 1:
                     inverse_norms(i - 1, 2)
+            if q == 0:
+                distance_end(WHOLE, TILES)
+            if 0 <= q - 2 < TILES:
+                chain_z_sq(q - 2)
+            group = time_group_ending_at(q - 2)
+            if group is not None:
+                time_coordinates(group[0], group[1])
+            if q == 0:
+                scale_rows(2)
+                turn_rows(2)
+            if q < TILES:
+                sum_h_squared(q, 0)
+            if q < TILES:
+                sum_h_squared(q, 1)
+            if q == 0:
+                nc.scalar.activation(out=t_exp[:], in_=t_arg[:], func=ACT.Exp)
+                nc.scalar.activation(out=t_exp_neg[:], in_=t_arg[:], func=ACT.Exp, scale=-1.0)
             if 0 <= q - 1 < TILES:
-                chain_shift(q - 1)
+                exponentials(q - 1)
+            if q == 0:
+                regroup(2)
+            if q == 1:
+                regroup(3)
+            if q >= 1 and q + 3 < TILES:
+                regroup(q + 3)
+            if 0 <= q - 2 < TILES:
+                finish(q - 2, 0)
+            if 0 <= q - 2 < TILES:
+                finish(q - 2, 1)
+            if q == 1:
+                quantise(2)
+            if q >= 1 and q + 2 < TILES:
+                quantise(q + 2)
+            if q >= 1 and q + 1 < TILES:
+                multiply(q + 1)
+            if q == 0:
+                scale_rows(3)
+                turn_rows(3)
+            if 0 <= q - 1 < TILES:
+                chain_y(q - 1)
+            if q < TILES:
+                chain_h_sq(q)
+                chain_r_inv(q)
+            if 0 <= q - 1 < TILES:
+                chain_x(q - 1)
             group = time_group_ending_at(q - 2)
             if group is not None:
                 place_times(group[0], group[1])
@@ -465,8 +462,6 @@ def tile_hyperboliclinearhyperboloid_kernel(tc, x, weight_words, weight_scales, 
             if group is not None:
                 for i in range(group[0], group[0] + group[1]):
                     store(i)
-            for i in scalings_of_period(q):
-                scale_rows(i)
             if q == 0:
                 bias_scalars()
             if q == 0:

@@ -42,8 +42,8 @@ def tile_hyperboliclinearhyperboloid_kernel(tc, x, weight_words, weight_scales, 
         keep = ctx.enter_context(tc.tile_pool(name="keep", bufs=1))
         work = ctx.enter_context(tc.tile_pool(name="work", bufs=3))
         junk = ctx.enter_context(tc.tile_pool(name="junk", bufs=2))
-        turn = ctx.enter_context(tc.psum_pool(name="turn", bufs=2))
-        prod = ctx.enter_context(tc.psum_pool(name="prod", bufs=6))
+        turn = ctx.enter_context(tc.psum_pool(name="turn", bufs=1))
+        prod = ctx.enter_context(tc.psum_pool(name="prod", bufs=7))
         ctx.enter_context(tc.manual_schedule())
 
         half = keep.tile([P, TILES], F32)
@@ -165,22 +165,25 @@ def tile_hyperboliclinearhyperboloid_kernel(tc, x, weight_words, weight_scales, 
         def quantise(i):
             nc.vector.quantize_mx(out=u_codes[:, i, :].bitcast(FP8X4), scales=u_scales[:, i, :], in_=grouped_of[i][:])
 
+        def multiply_half(i, nh):
+            h_bank = prod.tile([P, BANK], F32)
+            n_cols = slice(nh * BANK, (nh + 1) * BANK)
+            for g in range(PASSES):
+                m_cols = slice(g * P, (g + 1) * P)
+                nc.tensor.matmul_mx(
+                    out=h_bank[:],
+                    lhsT=u_codes[:, i, m_cols].bitcast(FP8X4),
+                    lhsT_scale=u_scales[:, i, m_cols],
+                    rhs=w_codes[:, g, n_cols].bitcast(FP8X4),
+                    rhs_scale=w_scales[:, g, n_cols],
+                    start=(g == 0),
+                    stop=(g == PASSES - 1),
+                )
+            bank_of[(i, nh)] = h_bank
+
         def multiply(i):
             for nh in range(HALVES):
-                h_bank = prod.tile([P, BANK], F32)
-                n_cols = slice(nh * BANK, (nh + 1) * BANK)
-                for g in range(PASSES):
-                    m_cols = slice(g * P, (g + 1) * P)
-                    nc.tensor.matmul_mx(
-                        out=h_bank[:],
-                        lhsT=u_codes[:, i, m_cols].bitcast(FP8X4),
-                        lhsT_scale=u_scales[:, i, m_cols],
-                        rhs=w_codes[:, g, n_cols].bitcast(FP8X4),
-                        rhs_scale=w_scales[:, g, n_cols],
-                        start=(g == 0),
-                        stop=(g == PASSES - 1),
-                    )
-                bank_of[(i, nh)] = h_bank
+                multiply_half(i, nh)
 
         def sum_h_bias(i, nh):
             hb_junk = junk.tile([P, BANK], F32)
@@ -386,6 +389,10 @@ def tile_hyperboliclinearhyperboloid_kernel(tc, x, weight_words, weight_scales, 
             return None
 
         for q in range(0, TILES + 2):
+            if q == 1:
+                regroup(3)
+            if q >= 2 and q + 1 < TILES:
+                multiply_half(q + 1, 0)
             if q >= 1 and q + 3 < TILES:
                 scale_rows(q + 3)
                 turn_rows(q + 3)
@@ -431,8 +438,6 @@ def tile_hyperboliclinearhyperboloid_kernel(tc, x, weight_words, weight_scales, 
                 exponentials(q - 1)
             if q == 0:
                 regroup(2)
-            if q == 1:
-                regroup(3)
             if q >= 1 and q + 3 < TILES:
                 regroup(q + 3)
             if 0 <= q - 2 < TILES:
@@ -443,8 +448,10 @@ def tile_hyperboliclinearhyperboloid_kernel(tc, x, weight_words, weight_scales, 
                 quantise(2)
             if q >= 1 and q + 2 < TILES:
                 quantise(q + 2)
+            if q == 1:
+                multiply_half(2, 0)
             if q >= 1 and q + 1 < TILES:
-                multiply(q + 1)
+                multiply_half(q + 1, 1)
             if q == 0:
                 scale_rows(3)
                 turn_rows(3)

@@ -139,6 +139,14 @@ def tile_hyperboliclinearhyperboloid_kernel(tc, x, weight_words, weight_scales, 
             nc.gpsimd.tensor_scalar(out=sp_sq_min[:, cols], in0=sp_sq[:, cols], scalar1=MIN_SQ, scalar2=None, op0=ALU.max)
             nc.gpsimd.tensor_tensor(out=inv_norm[:, cols], in0=sp_sq_min[:, cols], in1=neg_half[:, 0:n], op=ALU.pow)
 
+        def clamp_squares(i, n):
+            cols = slice(i, i + n)
+            nc.vector.tensor_scalar(out=sp_sq_min[:, cols], in0=sp_sq[:, cols], scalar1=MIN_SQ, scalar2=None, op0=ALU.max)
+
+        def inverse_roots(i, n):
+            cols = slice(i, i + n)
+            nc.gpsimd.tensor_tensor(out=inv_norm[:, cols], in0=sp_sq_min[:, cols], in1=neg_half[:, 0:n], op=ALU.pow)
+
         def scale_rows(i):
             u_bf = work.tile([P, K], BF16, align_bytes=64)
             nc.vector.tensor_scalar(
@@ -249,11 +257,12 @@ def tile_hyperboliclinearhyperboloid_kernel(tc, x, weight_words, weight_scales, 
                 out=col(z_sq, i), in_=col(y_neg, i), func=ACT.Square, scale=-2.0, bias=col(x_less_y, i)
             )
 
-        def time_coordinates(i, n):
+        def time_squares(i, n):
             cols = slice(i, i + n)
-            nc.gpsimd.tensor_scalar(
-                out=time_sq[:, cols], in0=z_sq[:, cols], scalar1=delta[:, 0:1], scalar2=1.0, op0=ALU.add, op1=ALU.add
-            )
+            nc.scalar.activation(out=time_sq[:, cols], in_=z_sq[:, cols], func=ACT.Identity, bias=delta_one[:, 0:1])
+
+        def time_roots(i, n):
+            cols = slice(i, i + n)
             nc.gpsimd.tensor_tensor(out=time_co[:, cols], in0=time_sq[:, cols], in1=half[:, 0:n], op=ALU.pow)
 
         def place_times(i, n):
@@ -310,6 +319,7 @@ def tile_hyperboliclinearhyperboloid_kernel(tc, x, weight_words, weight_scales, 
         neg_ct_sq = keep.tile([P, 1], F32)
         four_st_sq_bb = keep.tile([P, 1], F32)
         delta = keep.tile([P, 1], F32)
+        delta_one = keep.tile([P, 1], F32)
         b_term = keep.tile([P, N], F32)
 
         def bias_scalars():
@@ -335,6 +345,7 @@ def tile_hyperboliclinearhyperboloid_kernel(tc, x, weight_words, weight_scales, 
             nc.vector.tensor_scalar(
                 out=delta[:], in0=four_st_sq_bb[:], scalar1=0.25, scalar2=neg_ct_sq[:, 0:1], op0=ALU.mult, op1=ALU.add
             )
+            nc.vector.tensor_scalar(out=delta_one[:], in0=delta[:], scalar1=1.0, scalar2=None, op0=ALU.add)
             nc.vector.tensor_scalar(
                 out=b_term[:], in0=b_rows[:], scalar1=two_st[:, 0:1], scalar2=0.5, op0=ALU.mult, op1=ALU.mult
             )
@@ -396,6 +407,8 @@ def tile_hyperboliclinearhyperboloid_kernel(tc, x, weight_words, weight_scales, 
             if q >= 1 and q + 3 < TILES:
                 scale_rows(q + 3)
                 turn_rows(q + 3)
+            if 0 <= q - 2 < TILES:
+                chain_x(q - 2)
             if q < TILES:
                 sum_h_bias(q, 0)
             if q == 0:
@@ -415,15 +428,20 @@ def tile_hyperboliclinearhyperboloid_kernel(tc, x, weight_words, weight_scales, 
                 square_rows(i)
                 if i < 6:
                     inverse_norms(i, 1)
-                elif i % 2 == 1:
-                    inverse_norms(i - 1, 2)
-            if q == 0:
-                distance_end(WHOLE, TILES)
             if 0 <= q - 2 < TILES:
                 chain_z_sq(q - 2)
             group = time_group_ending_at(q - 2)
             if group is not None:
-                time_coordinates(group[0], group[1])
+                time_squares(group[0], group[1])
+            group = time_group_ending_at(q - 2)
+            if group is not None:
+                time_roots(group[0], group[1])
+            for i in squares_of_period(q):
+                if i >= 6 and i % 2 == 1:
+                    clamp_squares(i - 1, 2)
+                    inverse_roots(i - 1, 2)
+            if q == 0:
+                distance_end(WHOLE, TILES)
             if q == 0:
                 scale_rows(2)
                 turn_rows(2)
@@ -444,6 +462,9 @@ def tile_hyperboliclinearhyperboloid_kernel(tc, x, weight_words, weight_scales, 
                 finish(q - 2, 0)
             if 0 <= q - 2 < TILES:
                 finish(q - 2, 1)
+            if q < TILES:
+                chain_h_sq(q)
+                chain_r_inv(q)
             if q == 1:
                 quantise(2)
             if q >= 1 and q + 2 < TILES:
@@ -457,11 +478,6 @@ def tile_hyperboliclinearhyperboloid_kernel(tc, x, weight_words, weight_scales, 
                 turn_rows(3)
             if 0 <= q - 1 < TILES:
                 chain_y(q - 1)
-            if q < TILES:
-                chain_h_sq(q)
-                chain_r_inv(q)
-            if 0 <= q - 1 < TILES:
-                chain_x(q - 1)
             group = time_group_ending_at(q - 2)
             if group is not None:
                 place_times(group[0], group[1])

@@ -360,8 +360,13 @@ def tile_hyperboliclinearhyperboloid_kernel(tc, x, weight_words, weight_scales, 
         inverse_norms(1, 1)
         distance_sum(0, WHOLE)
         distance_end(0, WHOLE)
+        h_bank = prod.tile([P, BANK], F32)
+        for repeat in range(5):
+            nc.tensor.matmul(out=h_bank[:], lhsT=x_all[:, 0, 0:P], rhs=x_all[:, 0, P : P + BANK], start=True, stop=True)
         scale_rows(0)
         turn_rows(0)
+        for repeat in range(3):
+            nc.tensor.matmul(out=h_bank[:], lhsT=x_all[:, 0, 0:P], rhs=x_all[:, 0, P : P + BANK], start=True, stop=True)
         distance_start(WHOLE, TILES, x_time[:, WHOLE:TILES])
         scale_rows(1)
         turn_rows(1)

@@ -23,6 +23,8 @@ HALVES = N // BANK
 TILES = ROWS // P
 O_PITCH = 1032
 X_PITCH = 1040
+BEFORE_W = 5
+V_SQUARES = (3, 5)
 WHOLE = 2
 
 EPS = 1e-7
@@ -78,7 +80,8 @@ def tile_hyperboliclinearhyperboloid_kernel(tc, x, weight_words, weight_scales, 
                 out=x_time[:, WHOLE:TILES], in_=x[WHOLE * P : ROWS, 0:1].rearrange("(i p) o -> p (i o)", p=P)
             )
         nc.sync.dma_start(out=b_rows[:], in_=bias.rearrange("o n -> (o n)").partition_broadcast(P))
-        load_rows(WHOLE)
+        for i in range(WHOLE, BEFORE_W):
+            load_rows(i)
         for g in range(PASSES):
             nc.sync.dma_start(
                 out=w_codes[:, g, :].bitcast(I32),
@@ -90,7 +93,7 @@ def tile_hyperboliclinearhyperboloid_kernel(tc, x, weight_words, weight_scales, 
                     out=w_scales[32 * quad : 32 * quad + 4, g, :].bitcast(I32),
                     in_=weight_scales[g, 4 * quad : 4 * quad + 4, :].bitcast(I32),
                 )
-        for i in range(WHOLE + 1, TILES):
+        for i in range(BEFORE_W, TILES):
             load_rows(i)
 
         u_codes = keep.tile([P, TILES, PASSES * P], U32, align_bytes=64)
@@ -125,7 +128,7 @@ def tile_hyperboliclinearhyperboloid_kernel(tc, x, weight_words, weight_scales, 
 
         def square_rows(i):
             sp = spatial(i)
-            if i in (1, 4, 6):
+            if i in V_SQUARES:
                 sq_v = junk.tile([P, K], F32)
                 nc.vector.scalar_tensor_tensor(
                     out=sq_v[:], in0=sp, scalar=1.0, in1=sp, op0=ALU.mult, op1=ALU.mult, accum_out=col(sp_sq, i)
@@ -133,11 +136,6 @@ def tile_hyperboliclinearhyperboloid_kernel(tc, x, weight_words, weight_scales, 
             else:
                 sq_s = junk.tile([P, K], BF16)
                 nc.scalar.activation(out=sq_s[:], in_=sp, func=ACT.Square, accum_out=col(sp_sq, i))
-
-        def inverse_norms(i, n):
-            cols = slice(i, i + n)
-            nc.gpsimd.tensor_scalar(out=sp_sq_min[:, cols], in0=sp_sq[:, cols], scalar1=MIN_SQ, scalar2=None, op0=ALU.max)
-            nc.gpsimd.tensor_tensor(out=inv_norm[:, cols], in0=sp_sq_min[:, cols], in1=neg_half[:, 0:n], op=ALU.pow)
 
         def clamp_squares(i, n):
             cols = slice(i, i + n)
@@ -155,7 +153,12 @@ def tile_hyperboliclinearhyperboloid_kernel(tc, x, weight_words, weight_scales, 
             u_of[i] = u_bf
 
         def turn_rows(i):
-            turned = turn.tile([P, PASSES, 2, P], F32)
+            if i == 1:
+                h_bank = prod.tile([P, BANK], F32)
+                turned = h_bank[:].rearrange("p (g w r) -> p g w r", g=PASSES, w=2)
+            else:
+                t_bank = turn.tile([P, BANK], F32)
+                turned = t_bank[:].rearrange("p (g w r) -> p g w r", g=PASSES, w=2)
             u_words = u_of[i][:].bitcast(F32)
             for g in range(PASSES):
                 for w in range(2):
@@ -166,7 +169,7 @@ def tile_hyperboliclinearhyperboloid_kernel(tc, x, weight_words, weight_scales, 
             grouped = work.tile([P, PASSES * P * 4], BF16, align_bytes=64)
             nc.scalar.copy(
                 out=grouped[:].bitcast(F32).rearrange("p (g r w) -> p g r w", g=PASSES, w=2),
-                in_=turned_of[i][:].rearrange("p g w r -> p g r w"),
+                in_=turned_of[i].rearrange("p g w r -> p g r w"),
             )
             grouped_of[i] = grouped
 
@@ -288,8 +291,10 @@ def tile_hyperboliclinearhyperboloid_kernel(tc, x, weight_words, weight_scales, 
         ln_arg = keep.tile([P, TILES], F32)
         dist = keep.tile([P, TILES], F32)
 
-        def distance_start(a, b, times):
+        def clamp_times(a, b, times):
             nc.vector.tensor_scalar(out=theta[:, a:b], in0=times, scalar1=1.0 + EPS, scalar2=None, op0=ALU.max)
+
+        def distance_start(a, b):
             nc.vector.tensor_scalar(out=theta_less[:, a:b], in0=theta[:, a:b], scalar1=-1.0, scalar2=None, op0=ALU.add)
             nc.vector.scalar_tensor_tensor(
                 out=below[:, a:b], in0=theta[:, a:b], scalar=1.0, in1=theta_less[:, a:b], op0=ALU.add, op1=ALU.mult
@@ -353,47 +358,90 @@ def tile_hyperboliclinearhyperboloid_kernel(tc, x, weight_words, weight_scales, 
         warm = keep.tile([P, 1], F32)
         nc.scalar.activation(out=warm[:], in_=half[:, 0:1], func=ACT.Ln)
         square_rows(0)
-        distance_start(0, WHOLE, x_all[:, 0:WHOLE, 0])
-        distance_root(0, WHOLE)
-        inverse_norms(0, 1)
+        clamp_times(0, 1, x_all[:, 0:1, 0])
+        distance_start(0, 1)
+        distance_root(0, 1)
+        clamp_times(1, 2, x_all[:, 1:2, 0])
+        clamp_times(2, 6, x_time[:, 2:6])
+        distance_start(1, 6)
+        distance_sum(0, 1)
+        distance_end(0, 1)
+        clamp_squares(0, 1)
+        inverse_roots(0, 1)
+        distance_root(1, 6)
         square_rows(1)
-        inverse_norms(1, 1)
-        distance_sum(0, WHOLE)
-        distance_end(0, WHOLE)
-        h_bank = prod.tile([P, BANK], F32)
+        square_rows(2)
+        t_bank = turn.tile([P, BANK], F32)
         for repeat in range(5):
-            nc.tensor.matmul(out=h_bank[:], lhsT=x_all[:, 0, 0:P], rhs=x_all[:, 0, P : P + BANK], start=True, stop=True)
+            nc.tensor.matmul(out=t_bank[:], lhsT=x_all[:, 0, 0:P], rhs=x_all[:, 0, P : P + BANK], start=True, stop=True)
         scale_rows(0)
         turn_rows(0)
-        for repeat in range(3):
-            nc.tensor.matmul(out=h_bank[:], lhsT=x_all[:, 0, 0:P], rhs=x_all[:, 0, P : P + BANK], start=True, stop=True)
-        distance_start(WHOLE, TILES, x_time[:, WHOLE:TILES])
+        clamp_squares(1, 1)
+        inverse_roots(1, 1)
+        square_rows(3)
+        distance_sum(1, 6)
+        distance_end(1, 6)
+        clamp_squares(2, 2)
+        inverse_roots(2, 2)
         scale_rows(1)
         turn_rows(1)
+        regroup(0)
+        quantise(0)
+        scale_rows(2)
+        multiply(0)
+        turn_rows(2)
+        square_rows(4)
+        clamp_times(6, TILES, x_time[:, 6:TILES])
+        distance_start(6, TILES)
+        distance_root(6, TILES)
         b_junk = junk.tile([P, N], F32)
         nc.vector.scalar_tensor_tensor(
             out=b_junk[:], in0=b_rows[:], scalar=1.0, in1=b_rows[:], op0=ALU.mult, op1=ALU.mult, accum_out=b_sq[:]
         )
         nc.vector.tensor_scalar(out=b_sq_min[:], in0=b_sq[:], scalar1=1e-15, scalar2=None, op0=ALU.max)
-        distance_root(WHOLE, TILES)
         nc.gpsimd.tensor_tensor(out=t_raw[:], in0=b_sq_min[:], in1=half[:, 0:1], op=ALU.pow)
-        square_rows(2)
-        inverse_norms(2, 1)
-        regroup(0)
-        quantise(0)
-        multiply(0)
         regroup(1)
+        square_rows(5)
+        square_rows(6)
+        sum_h_bias(0, 0)
         quantise(1)
+        sum_h_bias(0, 1)
         multiply(1)
-
-        def squares_of_period(q):
-            if q == 0:
-                return [3, 4]
-            if q == 1:
-                return [5, 6]
-            if q >= 2 and q + 5 < TILES:
-                return [q + 5]
-            return []
+        clamp_squares(4, 1)
+        inverse_roots(4, 1)
+        scale_rows(3)
+        sum_h_squared(0, 0)
+        sum_h_squared(0, 1)
+        regroup(2)
+        turn_rows(3)
+        distance_sum(6, TILES)
+        distance_end(6, TILES)
+        nc.vector.tensor_scalar(out=t_arg[:], in0=t_raw[:], scalar1=1e-15, scalar2=MAX_ARG, op0=ALU.max, op1=ALU.min)
+        nc.vector.reciprocal(out=t_inv[:], in_=t_arg[:])
+        nc.scalar.activation(out=t_exp[:], in_=t_arg[:], func=ACT.Exp)
+        nc.scalar.activation(out=t_exp_neg[:], in_=t_arg[:], func=ACT.Exp, scale=-1.0)
+        chain_h_sq(0)
+        chain_r_inv(0)
+        sum_h_bias(1, 0)
+        sum_h_bias(1, 1)
+        quantise(2)
+        multiply(2)
+        scale_rows(4)
+        clamp_squares(5, 1)
+        inverse_roots(5, 1)
+        sum_h_squared(1, 0)
+        sum_h_squared(1, 1)
+        regroup(3)
+        turn_rows(4)
+        bias_scalars()
+        chain_after_r_inv(0)
+        exponentials(0)
+        chain_h_sq(1)
+        chain_r_inv(1)
+        bias_terms()
+        quantise(3)
+        regroup(4)
+        chain_y(0)
 
         def time_group_ending_at(i):
             if i < 0 or i >= TILES:
@@ -404,93 +452,49 @@ def tile_hyperboliclinearhyperboloid_kernel(tc, x, weight_words, weight_scales, 
                 return (i - 1, 2)
             return None
 
-        for q in range(0, TILES + 2):
-            if q == 1:
-                regroup(3)
-            if q >= 2 and q + 1 < TILES:
+        for q in range(2, TILES + 2):
+            if q + 1 < TILES:
                 multiply_half(q + 1, 0)
-            if q >= 1 and q + 3 < TILES:
+            if q + 3 < TILES:
                 scale_rows(q + 3)
                 turn_rows(q + 3)
-            if 0 <= q - 2 < TILES:
-                chain_x(q - 2)
+            chain_x(q - 2)
             if q < TILES:
                 sum_h_bias(q, 0)
-            if q == 0:
-                distance_sum(WHOLE, TILES)
-            if 0 <= q - 2 < TILES:
-                chain_coef(q - 2)
+            chain_coef(q - 2)
             if q < TILES:
                 sum_h_bias(q, 1)
-            if 0 <= q - 1 < TILES:
+            if q - 1 < TILES:
                 chain_after_r_inv(q - 1)
-            if q == 0:
-                nc.vector.tensor_scalar(
-                    out=t_arg[:], in0=t_raw[:], scalar1=1e-15, scalar2=MAX_ARG, op0=ALU.max, op1=ALU.min
-                )
-                nc.vector.reciprocal(out=t_inv[:], in_=t_arg[:])
-            for i in squares_of_period(q):
-                square_rows(i)
-                if i < 6:
-                    inverse_norms(i, 1)
-            if 0 <= q - 2 < TILES:
-                chain_z_sq(q - 2)
+            if q + 5 < TILES:
+                square_rows(q + 5)
+            chain_z_sq(q - 2)
             group = time_group_ending_at(q - 2)
             if group is not None:
                 time_squares(group[0], group[1])
-            group = time_group_ending_at(q - 2)
-            if group is not None:
                 time_roots(group[0], group[1])
-            for i in squares_of_period(q):
-                if i >= 6 and i % 2 == 1:
-                    clamp_squares(i - 1, 2)
-                    inverse_roots(i - 1, 2)
-            if q == 0:
-                distance_end(WHOLE, TILES)
-            if q == 0:
-                scale_rows(2)
-                turn_rows(2)
+            if q + 5 < TILES and (q + 5) % 2 == 1:
+                clamp_squares(q + 4, 2)
+                inverse_roots(q + 4, 2)
             if q < TILES:
                 sum_h_squared(q, 0)
-            if q < TILES:
                 sum_h_squared(q, 1)
-            if q == 0:
-                nc.scalar.activation(out=t_exp[:], in_=t_arg[:], func=ACT.Exp)
-                nc.scalar.activation(out=t_exp_neg[:], in_=t_arg[:], func=ACT.Exp, scale=-1.0)
-            if 0 <= q - 1 < TILES:
+            if q - 1 < TILES:
                 exponentials(q - 1)
-            if q == 0:
-                regroup(2)
-            if q >= 1 and q + 3 < TILES:
+            if q + 3 < TILES:
                 regroup(q + 3)
-            if 0 <= q - 2 < TILES:
-                finish(q - 2, 0)
-            if 0 <= q - 2 < TILES:
-                finish(q - 2, 1)
+            finish(q - 2, 0)
+            finish(q - 2, 1)
             if q < TILES:
                 chain_h_sq(q)
                 chain_r_inv(q)
-            if q == 1:
-                quantise(2)
-            if q >= 1 and q + 2 < TILES:
+            if q + 2 < TILES:
                 quantise(q + 2)
-            if q == 1:
-                multiply_half(2, 0)
-            if q >= 1 and q + 1 < TILES:
+            if q + 1 < TILES:
                 multiply_half(q + 1, 1)
-            if q == 0:
-                scale_rows(3)
-                turn_rows(3)
-            if 0 <= q - 1 < TILES:
+            if q - 1 < TILES:
                 chain_y(q - 1)
-            group = time_group_ending_at(q - 2)
             if group is not None:
                 place_times(group[0], group[1])
-            group = time_group_ending_at(q - 2)
-            if group is not None:
                 for i in range(group[0], group[0] + group[1]):
                     store(i)
-            if q == 0:
-                bias_scalars()
-            if q == 0:
-                bias_terms()

@@ -21,10 +21,13 @@ PASSES = K // K_PASS
 BANK = 512
 HALVES = N // BANK
 TILES = ROWS // P
-O_PITCH = 1032
+ROW_RUN = 8
+BLOCKS = TILES // ROW_RUN
+O_ROW = N + 1
+O_RUN = ROW_RUN * O_ROW
 X_PITCH = 1040
 BEFORE_W = 5
-V_SQUARES = (3, 5)
+V_SQUARES = (3, 5, 6)
 WHOLE = 2
 
 EPS = 1e-7
@@ -59,7 +62,7 @@ def tile_hyperboliclinearhyperboloid_kernel(tc, x, weight_words, weight_scales, 
         make_identity(nc, ident[:])
 
         x_all = keep.tile([P, TILES, X_PITCH], BF16)
-        x_time = keep.tile([P, TILES], BF16)
+        x_time = keep.tile([P, BLOCKS, 2 * ROW_RUN], BF16)
         b_rows = keep.tile([P, N], BF16)
 
         def spatial(i):
@@ -67,18 +70,24 @@ def tile_hyperboliclinearhyperboloid_kernel(tc, x, weight_words, weight_scales, 
                 return x_all[:, i, 1 : K + 1]
             return x_all[:, i, 0:K]
 
+        x_tiles = x.rearrange("(s p j) c -> s j p c", p=P, j=ROW_RUN)
+
         def load_rows(i):
+            rows = x_tiles[i // ROW_RUN][i % ROW_RUN]
             if i < WHOLE:
-                nc.sync.dma_start(out=x_all[:, i, 0 : K + 1], in_=x[i * P : (i + 1) * P, :])
+                nc.sync.dma_start(out=x_all[:, i, 0 : K + 1], in_=rows)
             else:
-                nc.sync.dma_start(out=x_all[:, i, 0:K], in_=x[i * P : (i + 1) * P, 1 : K + 1])
+                nc.sync.dma_start(out=x_all[:, i, 0:K], in_=rows[:, 1 : K + 1])
 
         for i in range(WHOLE):
             load_rows(i)
         with nc.allow_non_contiguous_dma(reason="one bfloat16 element of each row of x"):
-            nc.sync.dma_start(
-                out=x_time[:, WHOLE:TILES], in_=x[WHOLE * P : ROWS, 0:1].rearrange("(i p) o -> p (i o)", p=P)
-            )
+            for s in range(BLOCKS):
+                j0 = WHOLE if s == 0 else 0
+                nc.sync.dma_start(
+                    out=x_time[:, s, j0:ROW_RUN],
+                    in_=x_tiles[s][j0:ROW_RUN, :, 0:1].rearrange("j p o -> p (j o)"),
+                )
         nc.sync.dma_start(out=b_rows[:], in_=bias.rearrange("o n -> (o n)").partition_broadcast(P))
         for i in range(WHOLE, BEFORE_W):
             load_rows(i)
@@ -98,7 +107,8 @@ def tile_hyperboliclinearhyperboloid_kernel(tc, x, weight_words, weight_scales, 
 
         u_codes = keep.tile([P, TILES, PASSES * P], U32, align_bytes=64)
         u_scales = keep.tile([P, TILES, PASSES * P], U8, align_bytes=64)
-        o_all = keep.tile([P, TILES, O_PITCH], F32)
+        o_all = keep.tile([P, BLOCKS, O_RUN], F32)
+        out_runs = out.rearrange("(s p j) c -> s p (j c)", p=P, j=ROW_RUN)
 
         sp_sq = keep.tile([P, TILES], F32)
         sp_sq_min = keep.tile([P, TILES], F32)
@@ -269,11 +279,14 @@ def tile_hyperboliclinearhyperboloid_kernel(tc, x, weight_words, weight_scales, 
             nc.gpsimd.tensor_tensor(out=time_co[:, cols], in0=time_sq[:, cols], in1=half[:, 0:n], op=ALU.pow)
 
         def place_times(i, n):
-            nc.scalar.copy(out=o_all[:, i : i + n, 0], in_=time_co[:, i : i + n])
+            first = (i % ROW_RUN) * O_ROW
+            nc.scalar.copy(
+                out=o_all[:, i // ROW_RUN, first : first + (n - 1) * O_ROW + 1 : O_ROW], in_=time_co[:, i : i + n]
+            )
 
         def finish(i, nh):
             nc.vector.scalar_tensor_tensor(
-                out=o_all[:, i, 1 + nh * BANK : 1 + (nh + 1) * BANK],
+                out=o_all[:, i // ROW_RUN, (i % ROW_RUN) * O_ROW + 1 + nh * BANK : (i % ROW_RUN) * O_ROW + 1 + (nh + 1) * BANK],
                 in0=bank_of[(i, nh)][:],
                 scalar=col(coef, i),
                 in1=b_term[:, nh * BANK : (nh + 1) * BANK],
@@ -281,8 +294,16 @@ def tile_hyperboliclinearhyperboloid_kernel(tc, x, weight_words, weight_scales, 
                 op1=ALU.add,
             )
 
+        def store_run(s, a, b):
+            nc.sync.dma_start(out=out_runs[s][:, a:b], in_=o_all[:, s, a:b])
+
         def store(i):
-            nc.sync.dma_start(out=out[i * P : (i + 1) * P, :], in_=o_all[:, i, 0 : N + 1])
+            s, j = i // ROW_RUN, i % ROW_RUN
+            store_run(s, N * j, O_RUN if j == ROW_RUN - 1 else N * (j + 1))
+
+        def root_time(i, n):
+            time_squares(i, n)
+            time_roots(i, n)
 
         theta = keep.tile([P, TILES], F32)
         theta_less = keep.tile([P, TILES], F32)
@@ -362,8 +383,11 @@ def tile_hyperboliclinearhyperboloid_kernel(tc, x, weight_words, weight_scales, 
         distance_start(0, 1)
         distance_root(0, 1)
         clamp_times(1, 2, x_all[:, 1:2, 0])
-        clamp_times(2, 6, x_time[:, 2:6])
+        clamp_times(2, 6, x_time[:, 0, 2:6])
         distance_start(1, 6)
+        clamp_times(6, ROW_RUN, x_time[:, 0, 6:ROW_RUN])
+        clamp_times(ROW_RUN, TILES, x_time[:, 1, 0:ROW_RUN])
+        distance_start(6, TILES)
         distance_sum(0, 1)
         distance_end(0, 1)
         clamp_squares(0, 1)
@@ -381,28 +405,28 @@ def tile_hyperboliclinearhyperboloid_kernel(tc, x, weight_words, weight_scales, 
         square_rows(3)
         distance_sum(1, 6)
         distance_end(1, 6)
+        distance_root(6, TILES)
         clamp_squares(2, 2)
         inverse_roots(2, 2)
         scale_rows(1)
         turn_rows(1)
         regroup(0)
         quantise(0)
-        scale_rows(2)
         multiply(0)
-        turn_rows(2)
         square_rows(4)
-        clamp_times(6, TILES, x_time[:, 6:TILES])
-        distance_start(6, TILES)
-        distance_root(6, TILES)
         b_junk = junk.tile([P, N], F32)
         nc.vector.scalar_tensor_tensor(
             out=b_junk[:], in0=b_rows[:], scalar=1.0, in1=b_rows[:], op0=ALU.mult, op1=ALU.mult, accum_out=b_sq[:]
         )
         nc.vector.tensor_scalar(out=b_sq_min[:], in0=b_sq[:], scalar1=1e-15, scalar2=None, op0=ALU.max)
         nc.gpsimd.tensor_tensor(out=t_raw[:], in0=b_sq_min[:], in1=half[:, 0:1], op=ALU.pow)
+        distance_sum(6, TILES)
+        distance_end(6, TILES)
         regroup(1)
+        nc.scalar.activation(out=warm[:], in_=half[:, 0:1], func=ACT.Exp)
         square_rows(5)
-        square_rows(6)
+        scale_rows(2)
+        turn_rows(2)
         sum_h_bias(0, 0)
         quantise(1)
         sum_h_bias(0, 1)
@@ -414,8 +438,6 @@ def tile_hyperboliclinearhyperboloid_kernel(tc, x, weight_words, weight_scales, 
         sum_h_squared(0, 1)
         regroup(2)
         turn_rows(3)
-        distance_sum(6, TILES)
-        distance_end(6, TILES)
         nc.vector.tensor_scalar(out=t_arg[:], in0=t_raw[:], scalar1=1e-15, scalar2=MAX_ARG, op0=ALU.max, op1=ALU.min)
         nc.vector.reciprocal(out=t_inv[:], in_=t_arg[:])
         nc.scalar.activation(out=t_exp[:], in_=t_arg[:], func=ACT.Exp)
@@ -427,6 +449,7 @@ def tile_hyperboliclinearhyperboloid_kernel(tc, x, weight_words, weight_scales, 
         quantise(2)
         multiply(2)
         scale_rows(4)
+        square_rows(6)
         clamp_squares(5, 1)
         inverse_roots(5, 1)
         sum_h_squared(1, 0)
@@ -452,7 +475,7 @@ def tile_hyperboliclinearhyperboloid_kernel(tc, x, weight_words, weight_scales, 
                 return (i - 1, 2)
             return None
 
-        for q in range(2, TILES + 2):
+        for q in range(2, TILES - 1):
             if q + 1 < TILES:
                 multiply_half(q + 1, 0)
             if q + 3 < TILES:
@@ -498,3 +521,44 @@ def tile_hyperboliclinearhyperboloid_kernel(tc, x, weight_words, weight_scales, 
                 place_times(group[0], group[1])
                 for i in range(group[0], group[0] + group[1]):
                     store(i)
+
+        last = TILES - 1
+        chain_x(last - 2)
+        sum_h_bias(last, 0)
+        chain_coef(last - 2)
+        sum_h_bias(last, 1)
+        chain_after_r_inv(last - 1)
+        chain_z_sq(last - 2)
+        root_time(last - 3, 2)
+        sum_h_squared(last, 0)
+        sum_h_squared(last, 1)
+        exponentials(last - 1)
+        finish(last - 2, 0)
+        chain_h_sq(last)
+        chain_r_inv(last)
+        finish(last - 2, 1)
+        place_times(last - 3, 2)
+        store(last - 3)
+        store(last - 2)
+        chain_y(last - 1)
+        chain_x(last - 1)
+        chain_coef(last - 1)
+        chain_z_sq(last - 1)
+        root_time(last - 1, 1)
+        finish(last - 1, 0)
+        chain_after_r_inv(last)
+        exponentials(last)
+        finish(last - 1, 1)
+        place_times(last - 1, 1)
+        store(last - 1)
+        chain_y(last)
+        chain_x(last)
+        chain_coef(last)
+        chain_z_sq(last)
+        root_time(last, 1)
+        finish(last, 1)
+        half_way = (ROW_RUN - 1) * O_ROW + 1 + BANK
+        store_run(BLOCKS - 1, half_way, O_RUN)
+        finish(last, 0)
+        place_times(last, 1)
+        store_run(BLOCKS - 1, N * (ROW_RUN - 1), half_way)

@@ -25,6 +25,7 @@ ROW_RUN = 8
 BLOCKS = TILES // ROW_RUN
 O_ROW = N + 1
 O_RUN = ROW_RUN * O_ROW
+HALF_WAY = (ROW_RUN - 1) * O_ROW + 1 + BANK
 X_PITCH = 1040
 BEFORE_W = 5
 V_SQUARES = (3, 5, 6)
@@ -56,8 +57,8 @@ def tile_hyperboliclinearhyperboloid_kernel(tc, x, weight_words, weight_scales, 
         neg_half = keep.tile([P, TILES], F32)
         nc.vector.memset(neg_half[:], -0.5)
         w_codes = keep.tile([P, PASSES, N], U32, align_bytes=64)
-        w_scales = keep.tile([P, PASSES, N], U8, align_bytes=64)
-        nc.vector.memset(w_scales[:].rearrange("p g n -> p (g n)").bitcast(I32), 0)
+        w_scales = keep.tile([P, N], U8, align_bytes=64)
+        nc.vector.memset(w_scales[:].bitcast(I32), 0)
         ident = keep.tile([P, P], F32)
         make_identity(nc, ident[:])
 
@@ -96,12 +97,11 @@ def tile_hyperboliclinearhyperboloid_kernel(tc, x, weight_words, weight_scales, 
                 out=w_codes[:, g, :].bitcast(I32),
                 in_=weight_words[g].rearrange("p n t -> p (n t)").bitcast(I32),
             )
-        for g in range(PASSES):
-            for quad in range(4):
-                nc.sync.dma_start(
-                    out=w_scales[32 * quad : 32 * quad + 4, g, :].bitcast(I32),
-                    in_=weight_scales[g, 4 * quad : 4 * quad + 4, :].bitcast(I32),
-                )
+        for quad in range(4):
+            nc.sync.dma_start(
+                out=w_scales[32 * quad : 32 * quad + 4 * PASSES, :].bitcast(I32),
+                in_=weight_scales[:, 4 * quad : 4 * quad + 4, :].bitcast(I32),
+            )
         for i in range(BEFORE_W, TILES):
             load_rows(i)
 
@@ -196,7 +196,7 @@ def tile_hyperboliclinearhyperboloid_kernel(tc, x, weight_words, weight_scales, 
                     lhsT=u_codes[:, i, m_cols].bitcast(FP8X4),
                     lhsT_scale=u_scales[:, i, m_cols],
                     rhs=w_codes[:, g, n_cols].bitcast(FP8X4),
-                    rhs_scale=w_scales[:, g, n_cols],
+                    rhs_scale=w_scales[4 * g : P, n_cols],
                     start=(g == 0),
                     stop=(g == PASSES - 1),
                 )
@@ -279,9 +279,9 @@ def tile_hyperboliclinearhyperboloid_kernel(tc, x, weight_words, weight_scales, 
             nc.gpsimd.tensor_tensor(out=time_co[:, cols], in0=time_sq[:, cols], in1=half[:, 0:n], op=ALU.pow)
 
         def place_times(i, n):
-            first = (i % ROW_RUN) * O_ROW
             nc.scalar.copy(
-                out=o_all[:, i // ROW_RUN, first : first + (n - 1) * O_ROW + 1 : O_ROW], in_=time_co[:, i : i + n]
+                out=o_all[:].rearrange("p s c -> p (s c)")[:, i * O_ROW : (i + n - 1) * O_ROW + 1 : O_ROW],
+                in_=time_co[:, i : i + n],
             )
 
         def finish(i, nh):
@@ -301,9 +301,6 @@ def tile_hyperboliclinearhyperboloid_kernel(tc, x, weight_words, weight_scales, 
             s, j = i // ROW_RUN, i % ROW_RUN
             store_run(s, N * j, O_RUN if j == ROW_RUN - 1 else N * (j + 1))
 
-        def root_time(i, n):
-            time_squares(i, n)
-            time_roots(i, n)
 
         theta = keep.tile([P, TILES], F32)
         theta_less = keep.tile([P, TILES], F32)
@@ -314,9 +311,9 @@ def tile_hyperboliclinearhyperboloid_kernel(tc, x, weight_words, weight_scales, 
 
         def clamp_times(a, b, times):
             nc.vector.tensor_scalar(out=theta[:, a:b], in0=times, scalar1=1.0 + EPS, scalar2=None, op0=ALU.max)
+            nc.vector.tensor_scalar(out=theta_less[:, a:b], in0=times, scalar1=1.0 + EPS, scalar2=-1.0, op0=ALU.max, op1=ALU.add)
 
         def distance_start(a, b):
-            nc.vector.tensor_scalar(out=theta_less[:, a:b], in0=theta[:, a:b], scalar1=-1.0, scalar2=None, op0=ALU.add)
             nc.vector.scalar_tensor_tensor(
                 out=below[:, a:b], in0=theta[:, a:b], scalar=1.0, in1=theta_less[:, a:b], op0=ALU.add, op1=ALU.mult
             )
@@ -348,7 +345,7 @@ def tile_hyperboliclinearhyperboloid_kernel(tc, x, weight_words, weight_scales, 
         delta_one = keep.tile([P, 1], F32)
         b_term = keep.tile([P, N], F32)
 
-        def bias_scalars():
+        def bias_first():
             nc.vector.tensor_scalar(
                 out=half_ct[:], in0=t_exp[:], scalar1=t_exp_neg[:, 0:1], scalar2=0.25, op0=ALU.add, op1=ALU.mult
             )
@@ -356,11 +353,11 @@ def tile_hyperboliclinearhyperboloid_kernel(tc, x, weight_words, weight_scales, 
                 out=two_st[:], in0=t_exp[:], scalar1=t_exp_neg[:, 0:1], scalar2=t_inv[:, 0:1],
                 op0=ALU.subtract, op1=ALU.mult,
             )
+
+        def bias_second():
             nc.vector.tensor_scalar(out=neg_half_ct[:], in0=half_ct[:], scalar1=-1.0, scalar2=None, op0=ALU.mult)
             nc.vector.tensor_scalar(out=half_st[:], in0=two_st[:], scalar1=0.25, scalar2=None, op0=ALU.mult)
             nc.vector.tensor_scalar(out=st[:], in0=two_st[:], scalar1=0.5, scalar2=None, op0=ALU.mult)
-
-        def bias_terms():
             nc.vector.tensor_scalar(
                 out=neg_ct_sq[:], in0=half_ct[:], scalar1=half_ct[:, 0:1], scalar2=-4.0, op0=ALU.mult, op1=ALU.mult
             )
@@ -368,10 +365,16 @@ def tile_hyperboliclinearhyperboloid_kernel(tc, x, weight_words, weight_scales, 
                 out=four_st_sq_bb[:], in0=two_st[:], scalar1=two_st[:, 0:1], scalar2=b_sq[:, 0:1],
                 op0=ALU.mult, op1=ALU.mult,
             )
+
+        def bias_third():
             nc.vector.tensor_scalar(
                 out=delta[:], in0=four_st_sq_bb[:], scalar1=0.25, scalar2=neg_ct_sq[:, 0:1], op0=ALU.mult, op1=ALU.add
             )
+
+        def bias_fourth():
             nc.vector.tensor_scalar(out=delta_one[:], in0=delta[:], scalar1=1.0, scalar2=None, op0=ALU.add)
+
+        def bias_row():
             nc.vector.tensor_scalar(
                 out=b_term[:], in0=b_rows[:], scalar1=two_st[:, 0:1], scalar2=0.5, op0=ALU.mult, op1=ALU.mult
             )
@@ -383,23 +386,24 @@ def tile_hyperboliclinearhyperboloid_kernel(tc, x, weight_words, weight_scales, 
         distance_start(0, 1)
         distance_root(0, 1)
         clamp_times(1, 2, x_all[:, 1:2, 0])
-        clamp_times(2, 6, x_time[:, 0, 2:6])
-        distance_start(1, 6)
-        clamp_times(6, ROW_RUN, x_time[:, 0, 6:ROW_RUN])
+        clamp_times(2, ROW_RUN, x_time[:, 0, 2:ROW_RUN])
         clamp_times(ROW_RUN, TILES, x_time[:, 1, 0:ROW_RUN])
-        distance_start(6, TILES)
-        distance_sum(0, 1)
-        distance_end(0, 1)
         clamp_squares(0, 1)
         inverse_roots(0, 1)
-        distance_root(1, 6)
+        distance_start(1, TILES)
         square_rows(1)
+        distance_sum(0, 1)
+        distance_end(0, 1)
+        distance_root(1, 6)
         square_rows(2)
+        h_bank = prod.tile([P, BANK], F32)
         t_bank = turn.tile([P, BANK], F32)
         for repeat in range(5):
             nc.tensor.matmul(out=t_bank[:], lhsT=x_all[:, 0, 0:P], rhs=x_all[:, 0, P : P + BANK], start=True, stop=True)
         scale_rows(0)
         turn_rows(0)
+        for repeat in range(3):
+            nc.tensor.matmul(out=h_bank[:], lhsT=x_all[:, 0, 0:P], rhs=x_all[:, 0, P : P + BANK], start=True, stop=True)
         clamp_squares(1, 1)
         inverse_roots(1, 1)
         square_rows(3)
@@ -418,64 +422,70 @@ def tile_hyperboliclinearhyperboloid_kernel(tc, x, weight_words, weight_scales, 
         nc.vector.scalar_tensor_tensor(
             out=b_junk[:], in0=b_rows[:], scalar=1.0, in1=b_rows[:], op0=ALU.mult, op1=ALU.mult, accum_out=b_sq[:]
         )
-        nc.vector.tensor_scalar(out=b_sq_min[:], in0=b_sq[:], scalar1=1e-15, scalar2=None, op0=ALU.max)
-        nc.gpsimd.tensor_tensor(out=t_raw[:], in0=b_sq_min[:], in1=half[:, 0:1], op=ALU.pow)
         distance_sum(6, TILES)
         distance_end(6, TILES)
+        nc.vector.tensor_scalar(out=b_sq_min[:], in0=b_sq[:], scalar1=1e-15, scalar2=None, op0=ALU.max)
+        nc.gpsimd.tensor_tensor(out=t_raw[:], in0=b_sq_min[:], in1=half[:, 0:1], op=ALU.pow)
         regroup(1)
         nc.scalar.activation(out=warm[:], in_=half[:, 0:1], func=ACT.Exp)
-        square_rows(5)
-        scale_rows(2)
-        turn_rows(2)
         sum_h_bias(0, 0)
         quantise(1)
         sum_h_bias(0, 1)
         multiply(1)
+        scale_rows(2)
+        turn_rows(2)
+        nc.vector.tensor_scalar(out=t_arg[:], in0=t_raw[:], scalar1=1e-15, scalar2=MAX_ARG, op0=ALU.max, op1=ALU.min)
         clamp_squares(4, 1)
         inverse_roots(4, 1)
         scale_rows(3)
+        nc.vector.reciprocal(out=t_inv[:], in_=t_arg[:])
+        nc.scalar.activation(out=t_exp[:], in_=t_arg[:], func=ACT.Exp)
+        nc.scalar.activation(out=t_exp_neg[:], in_=t_arg[:], func=ACT.Exp, scale=-1.0)
         sum_h_squared(0, 0)
         sum_h_squared(0, 1)
         regroup(2)
         turn_rows(3)
-        nc.vector.tensor_scalar(out=t_arg[:], in0=t_raw[:], scalar1=1e-15, scalar2=MAX_ARG, op0=ALU.max, op1=ALU.min)
-        nc.vector.reciprocal(out=t_inv[:], in_=t_arg[:])
-        nc.scalar.activation(out=t_exp[:], in_=t_arg[:], func=ACT.Exp)
-        nc.scalar.activation(out=t_exp_neg[:], in_=t_arg[:], func=ACT.Exp, scale=-1.0)
+        square_rows(5)
         chain_h_sq(0)
         chain_r_inv(0)
+        bias_first()
         sum_h_bias(1, 0)
+        bias_second()
         sum_h_bias(1, 1)
+        bias_third()
         quantise(2)
         multiply(2)
+        bias_fourth()
         scale_rows(4)
-        square_rows(6)
         clamp_squares(5, 1)
         inverse_roots(5, 1)
+        chain_after_r_inv(0)
+        square_rows(6)
         sum_h_squared(1, 0)
         sum_h_squared(1, 1)
         regroup(3)
         turn_rows(4)
-        bias_scalars()
-        chain_after_r_inv(0)
         exponentials(0)
+        square_rows(7)
         chain_h_sq(1)
         chain_r_inv(1)
-        bias_terms()
+        bias_row()
         quantise(3)
+        clamp_squares(6, 2)
+        inverse_roots(6, 2)
         regroup(4)
         chain_y(0)
 
         def time_group_ending_at(i):
             if i < 0 or i >= TILES:
                 return None
-            if i >= TILES - 2:
+            if i == 0 or i >= TILES - 3:
                 return (i, 1)
-            if i % 2 == 1:
+            if i % 2 == 0:
                 return (i - 1, 2)
             return None
 
-        for q in range(2, TILES - 1):
+        for q in range(2, TILES + 2):
             if q + 1 < TILES:
                 multiply_half(q + 1, 0)
             if q + 3 < TILES:
@@ -487,27 +497,35 @@ def tile_hyperboliclinearhyperboloid_kernel(tc, x, weight_words, weight_scales, 
             chain_coef(q - 2)
             if q < TILES:
                 sum_h_bias(q, 1)
-            if q - 1 < TILES:
+            if q - 1 < TILES - 1:
                 chain_after_r_inv(q - 1)
-            if q + 5 < TILES:
-                square_rows(q + 5)
+            if q + 6 < TILES:
+                square_rows(q + 6)
             chain_z_sq(q - 2)
             group = time_group_ending_at(q - 2)
             if group is not None:
                 time_squares(group[0], group[1])
                 time_roots(group[0], group[1])
-            if q + 5 < TILES and (q + 5) % 2 == 1:
-                clamp_squares(q + 4, 2)
-                inverse_roots(q + 4, 2)
+            if q + 6 < TILES and (q + 6) % 2 == 1:
+                clamp_squares(q + 5, 2)
+                inverse_roots(q + 5, 2)
             if q < TILES:
                 sum_h_squared(q, 0)
                 sum_h_squared(q, 1)
-            if q - 1 < TILES:
+            if q - 1 < TILES - 1:
                 exponentials(q - 1)
             if q + 3 < TILES:
                 regroup(q + 3)
-            finish(q - 2, 0)
-            finish(q - 2, 1)
+            if q - 2 == TILES - 1:
+                finish(q - 2, 1)
+                store_run(BLOCKS - 1, HALF_WAY, O_RUN)
+                finish(q - 2, 0)
+            else:
+                finish(q - 2, 0)
+                if q - 1 == TILES - 1:
+                    chain_after_r_inv(q - 1)
+                    exponentials(q - 1)
+                finish(q - 2, 1)
             if q < TILES:
                 chain_h_sq(q)
                 chain_r_inv(q)
@@ -520,45 +538,7 @@ def tile_hyperboliclinearhyperboloid_kernel(tc, x, weight_words, weight_scales, 
             if group is not None:
                 place_times(group[0], group[1])
                 for i in range(group[0], group[0] + group[1]):
-                    store(i)
-
-        last = TILES - 1
-        chain_x(last - 2)
-        sum_h_bias(last, 0)
-        chain_coef(last - 2)
-        sum_h_bias(last, 1)
-        chain_after_r_inv(last - 1)
-        chain_z_sq(last - 2)
-        root_time(last - 3, 2)
-        sum_h_squared(last, 0)
-        sum_h_squared(last, 1)
-        exponentials(last - 1)
-        finish(last - 2, 0)
-        chain_h_sq(last)
-        chain_r_inv(last)
-        finish(last - 2, 1)
-        place_times(last - 3, 2)
-        store(last - 3)
-        store(last - 2)
-        chain_y(last - 1)
-        chain_x(last - 1)
-        chain_coef(last - 1)
-        chain_z_sq(last - 1)
-        root_time(last - 1, 1)
-        finish(last - 1, 0)
-        chain_after_r_inv(last)
-        exponentials(last)
-        finish(last - 1, 1)
-        place_times(last - 1, 1)
-        store(last - 1)
-        chain_y(last)
-        chain_x(last)
-        chain_coef(last)
-        chain_z_sq(last)
-        root_time(last, 1)
-        finish(last, 1)
-        half_way = (ROW_RUN - 1) * O_ROW + 1 + BANK
-        store_run(BLOCKS - 1, half_way, O_RUN)
-        finish(last, 0)
-        place_times(last, 1)
-        store_run(BLOCKS - 1, N * (ROW_RUN - 1), half_way)
+                    if i == TILES - 1:
+                        store_run(BLOCKS - 1, N * (ROW_RUN - 1), HALF_WAY)
+                    else:
+                        store(i)

@@ -27,6 +27,7 @@ O_ROW = N + 1
 O_RUN = ROW_RUN * O_ROW
 HALF_WAY = (ROW_RUN - 1) * O_ROW + 1 + BANK
 X_PITCH = 1040
+V_COPIES = (4,)
 BEFORE_W = 5
 V_SQUARES = (3, 5, 6)
 WHOLE = 2
@@ -126,6 +127,8 @@ def tile_hyperboliclinearhyperboloid_kernel(tc, x, weight_words, weight_scales, 
         r_exp_neg = keep.tile([P, TILES], F32)
         y_neg = keep.tile([P, TILES], F32)
         x_less_y = keep.tile([P, TILES], F32)
+        x_less_shift = keep.tile([P, TILES], F32)
+        x_alone = keep.tile([P, TILES], F32)
         coef = keep.tile([P, TILES], F32)
         z_sq = keep.tile([P, TILES], F32)
         time_sq = keep.tile([P, TILES], F32)
@@ -177,7 +180,8 @@ def tile_hyperboliclinearhyperboloid_kernel(tc, x, weight_words, weight_scales, 
 
         def regroup(i):
             grouped = work.tile([P, PASSES * P * 4], BF16, align_bytes=64)
-            nc.scalar.copy(
+            copy = nc.vector.tensor_copy if i in V_COPIES else nc.scalar.copy
+            copy(
                 out=grouped[:].bitcast(F32).rearrange("p (g r w) -> p g r w", g=PASSES, w=2),
                 in_=turned_of[i].rearrange("p g w r -> p g r w"),
             )
@@ -264,6 +268,27 @@ def tile_hyperboliclinearhyperboloid_kernel(tc, x, weight_words, weight_scales, 
                 out=col(coef, i), in0=col(x_less_y, i), scalar1=col(shift, i), scalar2=col(r_inv, i),
                 op0=ALU.subtract, op1=ALU.mult,
             )
+
+        def chain_pair(i):
+            nc.vector.tensor_scalar(
+                out=col(y_neg, i), in0=col(r_exp_neg, i), scalar1=col(y_fac, i), scalar2=None, op0=ALU.mult
+            )
+            nc.vector.tensor_scalar(
+                out=col(x_less_shift, i), in0=col(r_exp, i), scalar1=col(x_fac, i), scalar2=col(shift, i),
+                op0=ALU.mult, op1=ALU.subtract,
+            )
+            nc.vector.tensor_scalar(
+                out=col(x_alone, i), in0=col(r_exp, i), scalar1=col(x_fac, i), scalar2=None, op0=ALU.mult
+            )
+
+        def chain_coef_of_pair(i):
+            nc.vector.tensor_scalar(
+                out=col(coef, i), in0=col(x_less_shift, i), scalar1=col(y_neg, i), scalar2=col(r_inv, i),
+                op0=ALU.add, op1=ALU.mult,
+            )
+
+        def chain_z_sq_of_pair(i):
+            nc.scalar.activation(out=col(z_sq, i), in_=col(y_neg, i), func=ACT.Square, scale=-1.0, bias=col(x_alone, i))
 
         def chain_z_sq(i):
             nc.scalar.activation(
@@ -422,11 +447,11 @@ def tile_hyperboliclinearhyperboloid_kernel(tc, x, weight_words, weight_scales, 
         nc.vector.scalar_tensor_tensor(
             out=b_junk[:], in0=b_rows[:], scalar=1.0, in1=b_rows[:], op0=ALU.mult, op1=ALU.mult, accum_out=b_sq[:]
         )
+        regroup(1)
         distance_sum(6, TILES)
         distance_end(6, TILES)
         nc.vector.tensor_scalar(out=b_sq_min[:], in0=b_sq[:], scalar1=1e-15, scalar2=None, op0=ALU.max)
         nc.gpsimd.tensor_tensor(out=t_raw[:], in0=b_sq_min[:], in1=half[:, 0:1], op=ALU.pow)
-        regroup(1)
         nc.scalar.activation(out=warm[:], in_=half[:, 0:1], func=ACT.Exp)
         sum_h_bias(0, 0)
         quantise(1)
@@ -485,20 +510,16 @@ def tile_hyperboliclinearhyperboloid_kernel(tc, x, weight_words, weight_scales, 
                 return (i - 1, 2)
             return None
 
-        for q in range(2, TILES + 2):
-            if q + 1 < TILES:
-                multiply_half(q + 1, 0)
+        for q in range(2, TILES - 1):
+            multiply_half(q + 1, 0)
             if q + 3 < TILES:
                 scale_rows(q + 3)
                 turn_rows(q + 3)
             chain_x(q - 2)
-            if q < TILES:
-                sum_h_bias(q, 0)
+            sum_h_bias(q, 0)
             chain_coef(q - 2)
-            if q < TILES:
-                sum_h_bias(q, 1)
-            if q - 1 < TILES - 1:
-                chain_after_r_inv(q - 1)
+            sum_h_bias(q, 1)
+            chain_after_r_inv(q - 1)
             if q + 6 < TILES:
                 square_rows(q + 6)
             chain_z_sq(q - 2)
@@ -509,36 +530,60 @@ def tile_hyperboliclinearhyperboloid_kernel(tc, x, weight_words, weight_scales, 
             if q + 6 < TILES and (q + 6) % 2 == 1:
                 clamp_squares(q + 5, 2)
                 inverse_roots(q + 5, 2)
-            if q < TILES:
-                sum_h_squared(q, 0)
-                sum_h_squared(q, 1)
-            if q - 1 < TILES - 1:
-                exponentials(q - 1)
+            sum_h_squared(q, 0)
+            sum_h_squared(q, 1)
+            exponentials(q - 1)
             if q + 3 < TILES:
                 regroup(q + 3)
-            if q - 2 == TILES - 1:
-                finish(q - 2, 1)
-                store_run(BLOCKS - 1, HALF_WAY, O_RUN)
-                finish(q - 2, 0)
-            else:
-                finish(q - 2, 0)
-                if q - 1 == TILES - 1:
-                    chain_after_r_inv(q - 1)
-                    exponentials(q - 1)
-                finish(q - 2, 1)
-            if q < TILES:
-                chain_h_sq(q)
-                chain_r_inv(q)
+            finish(q - 2, 0)
+            finish(q - 2, 1)
+            chain_h_sq(q)
+            chain_r_inv(q)
             if q + 2 < TILES:
                 quantise(q + 2)
-            if q + 1 < TILES:
-                multiply_half(q + 1, 1)
-            if q - 1 < TILES:
-                chain_y(q - 1)
+            multiply_half(q + 1, 1)
+            chain_y(q - 1)
             if group is not None:
                 place_times(group[0], group[1])
                 for i in range(group[0], group[0] + group[1]):
-                    if i == TILES - 1:
-                        store_run(BLOCKS - 1, N * (ROW_RUN - 1), HALF_WAY)
-                    else:
-                        store(i)
+                    store(i)
+
+        last = TILES - 1
+        chain_x(last - 2)
+        sum_h_bias(last, 0)
+        chain_coef(last - 2)
+        sum_h_bias(last, 1)
+        chain_after_r_inv(last - 1)
+        chain_z_sq(last - 2)
+        time_squares(last - 2, 1)
+        time_roots(last - 2, 1)
+        sum_h_squared(last, 0)
+        exponentials(last - 1)
+        sum_h_squared(last, 1)
+        finish(last - 2, 0)
+        chain_pair(last - 1)
+        finish(last - 2, 1)
+        chain_coef_of_pair(last - 1)
+        chain_h_sq(last)
+        chain_r_inv(last)
+        place_times(last - 2, 1)
+        store(last - 2)
+        chain_z_sq_of_pair(last - 1)
+        time_squares(last - 1, 1)
+        time_roots(last - 1, 1)
+        finish(last - 1, 0)
+        finish(last - 1, 1)
+        chain_after_r_inv(last)
+        exponentials(last)
+        place_times(last - 1, 1)
+        store(last - 1)
+        chain_pair(last)
+        chain_coef_of_pair(last)
+        chain_z_sq_of_pair(last)
+        time_squares(last, 1)
+        time_roots(last, 1)
+        finish(last, 1)
+        store_run(BLOCKS - 1, HALF_WAY, O_RUN)
+        finish(last, 0)
+        place_times(last, 1)
+        store_run(BLOCKS - 1, N * (ROW_RUN - 1), HALF_WAY)

@@ -253,9 +253,7 @@ def tile_hyperboliclinearhyperboloid_kernel(tc, x, weight_words, weight_scales, 
             nc.scalar.activation(out=col(shift, i), in_=col(along, i), func=ACT.Identity, scale=st[:, 0:1])
 
         def chain_y(i):
-            nc.vector.tensor_scalar(
-                out=col(y_neg, i), in0=col(r_exp_neg, i), scalar1=col(y_fac, i), scalar2=None, op0=ALU.mult
-            )
+            nc.scalar.activation(out=col(y_neg, i), in_=col(r_exp_neg, i), func=ACT.Identity, scale=col(y_fac, i))
 
         def chain_x(i):
             nc.vector.tensor_scalar(
@@ -535,6 +533,7 @@ def tile_hyperboliclinearhyperboloid_kernel(tc, x, weight_words, weight_scales, 
             exponentials(q - 1)
             if q + 3 < TILES:
                 regroup(q + 3)
+            chain_y(q - 1)
             finish(q - 2, 0)
             finish(q - 2, 1)
             chain_h_sq(q)
@@ -542,7 +541,6 @@ def tile_hyperboliclinearhyperboloid_kernel(tc, x, weight_words, weight_scales, 
             if q + 2 < TILES:
                 quantise(q + 2)
             multiply_half(q + 1, 1)
-            chain_y(q - 1)
             if group is not None:
                 place_times(group[0], group[1])
                 for i in range(group[0], group[0] + group[1]):

@@ -256,9 +256,8 @@ def tile_hyperboliclinearhyperboloid_kernel(tc, x, weight_words, weight_scales, 
             nc.scalar.activation(out=col(y_neg, i), in_=col(r_exp_neg, i), func=ACT.Identity, scale=col(y_fac, i))
 
         def chain_x(i):
-            nc.vector.tensor_scalar(
-                out=col(x_less_y, i), in0=col(r_exp, i), scalar1=col(x_fac, i), scalar2=col(y_neg, i),
-                op0=ALU.mult, op1=ALU.add,
+            nc.scalar.activation(
+                out=col(x_less_y, i), in_=col(r_exp, i), func=ACT.Identity, scale=col(x_fac, i), bias=col(y_neg, i)
             )
 
         def chain_coef(i):
@@ -496,8 +495,9 @@ def tile_hyperboliclinearhyperboloid_kernel(tc, x, weight_words, weight_scales, 
         quantise(3)
         clamp_squares(6, 2)
         inverse_roots(6, 2)
-        regroup(4)
         chain_y(0)
+        regroup(4)
+        chain_x(0)
 
         def time_group_ending_at(i):
             if i < 0 or i >= TILES:
@@ -513,7 +513,6 @@ def tile_hyperboliclinearhyperboloid_kernel(tc, x, weight_words, weight_scales, 
             if q + 3 < TILES:
                 scale_rows(q + 3)
                 turn_rows(q + 3)
-            chain_x(q - 2)
             sum_h_bias(q, 0)
             chain_coef(q - 2)
             sum_h_bias(q, 1)
@@ -529,11 +528,12 @@ def tile_hyperboliclinearhyperboloid_kernel(tc, x, weight_words, weight_scales, 
                 clamp_squares(q + 5, 2)
                 inverse_roots(q + 5, 2)
             sum_h_squared(q, 0)
-            sum_h_squared(q, 1)
             exponentials(q - 1)
+            sum_h_squared(q, 1)
+            chain_y(q - 1)
             if q + 3 < TILES:
                 regroup(q + 3)
-            chain_y(q - 1)
+            chain_x(q - 1)
             finish(q - 2, 0)
             finish(q - 2, 1)
             chain_h_sq(q)
@@ -547,7 +547,6 @@ def tile_hyperboliclinearhyperboloid_kernel(tc, x, weight_words, weight_scales, 
                     store(i)
 
         last = TILES - 1
-        chain_x(last - 2)
         sum_h_bias(last, 0)
         chain_coef(last - 2)
         sum_h_bias(last, 1)

@@ -28,6 +28,7 @@ O_RUN = ROW_RUN * O_ROW
 HALF_WAY = (ROW_RUN - 1) * O_ROW + 1 + BANK
 X_PITCH = 1040
 V_COPIES = (4,)
+PLAIN = 2
 BEFORE_W = 5
 V_SQUARES = (3, 5, 6)
 WHOLE = 2
@@ -213,7 +214,8 @@ def tile_hyperboliclinearhyperboloid_kernel(tc, x, weight_words, weight_scales, 
         def sum_h_bias(i, nh):
             hb_junk = junk.tile([P, BANK], F32)
             nc.vector.scalar_tensor_tensor(
-                out=hb_junk[:], in0=bank_of[(i, nh)][:], scalar=1.0, in1=b_rows[:, nh * BANK : (nh + 1) * BANK],
+                out=hb_junk[:], in0=bank_of[(i, nh)][:], scalar=1.0 if i < PLAIN else st[:, 0:1],
+                in1=b_rows[:, nh * BANK : (nh + 1) * BANK],
                 op0=ALU.mult, op1=ALU.mult, accum_out=h_b_parts[:, i, nh : nh + 1],
             )
 
@@ -241,16 +243,21 @@ def tile_hyperboliclinearhyperboloid_kernel(tc, x, weight_words, weight_scales, 
                 op0=ALU.add, op1=ALU.mult,
             )
 
+        def shift_of(i):
+            return col(shift, i) if i < PLAIN else col(along, i)
+
         def exponentials(i):
+            half_of = half_st[:, 0:1] if i < PLAIN else 0.5
             nc.scalar.activation(out=col(r_exp, i), in_=col(r_arg, i), func=ACT.Exp)
             nc.scalar.activation(out=col(r_exp_neg, i), in_=col(r_arg, i), func=ACT.Exp, scale=-1.0)
             nc.scalar.activation(
-                out=col(y_fac, i), in_=col(along, i), func=ACT.Identity, scale=half_st[:, 0:1], bias=neg_half_ct[:, 0:1]
+                out=col(y_fac, i), in_=col(along, i), func=ACT.Identity, scale=half_of, bias=neg_half_ct[:, 0:1]
             )
             nc.scalar.activation(
-                out=col(x_fac, i), in_=col(along, i), func=ACT.Identity, scale=half_st[:, 0:1], bias=half_ct[:, 0:1]
+                out=col(x_fac, i), in_=col(along, i), func=ACT.Identity, scale=half_of, bias=half_ct[:, 0:1]
             )
-            nc.scalar.activation(out=col(shift, i), in_=col(along, i), func=ACT.Identity, scale=st[:, 0:1])
+            if i < PLAIN:
+                nc.scalar.activation(out=col(shift, i), in_=col(along, i), func=ACT.Identity, scale=st[:, 0:1])
 
         def chain_y(i):
             nc.scalar.activation(out=col(y_neg, i), in_=col(r_exp_neg, i), func=ACT.Identity, scale=col(y_fac, i))
@@ -262,7 +269,7 @@ def tile_hyperboliclinearhyperboloid_kernel(tc, x, weight_words, weight_scales, 
 
         def chain_coef(i):
             nc.vector.tensor_scalar(
-                out=col(coef, i), in0=col(x_less_y, i), scalar1=col(shift, i), scalar2=col(r_inv, i),
+                out=col(coef, i), in0=col(x_less_y, i), scalar1=shift_of(i), scalar2=col(r_inv, i),
                 op0=ALU.subtract, op1=ALU.mult,
             )
 
@@ -271,7 +278,7 @@ def tile_hyperboliclinearhyperboloid_kernel(tc, x, weight_words, weight_scales, 
                 out=col(y_neg, i), in0=col(r_exp_neg, i), scalar1=col(y_fac, i), scalar2=None, op0=ALU.mult
             )
             nc.vector.tensor_scalar(
-                out=col(x_less_shift, i), in0=col(r_exp, i), scalar1=col(x_fac, i), scalar2=col(shift, i),
+                out=col(x_less_shift, i), in0=col(r_exp, i), scalar1=col(x_fac, i), scalar2=shift_of(i),
                 op0=ALU.mult, op1=ALU.subtract,
             )
             nc.vector.tensor_scalar(

@@ -28,6 +28,7 @@ O_RUN = ROW_RUN * O_ROW
 HALF_WAY = (ROW_RUN - 1) * O_ROW + 1 + BANK
 X_PITCH = 1040
 V_COPIES = (4,)
+OWN_INPUTS = 8
 PLAIN = 2
 BEFORE_W = 5
 V_SQUARES = (3, 5, 6)
@@ -153,7 +154,8 @@ def tile_hyperboliclinearhyperboloid_kernel(tc, x, weight_words, weight_scales, 
 
         def clamp_squares(i, n):
             cols = slice(i, i + n)
-            nc.vector.tensor_scalar(out=sp_sq_min[:, cols], in0=sp_sq[:, cols], scalar1=MIN_SQ, scalar2=None, op0=ALU.max)
+            engine = nc.vector if i < OWN_INPUTS else nc.gpsimd
+            engine.tensor_scalar(out=sp_sq_min[:, cols], in0=sp_sq[:, cols], scalar1=MIN_SQ, scalar2=None, op0=ALU.max)
 
         def inverse_roots(i, n):
             cols = slice(i, i + n)
@@ -226,7 +228,8 @@ def tile_hyperboliclinearhyperboloid_kernel(tc, x, weight_words, weight_scales, 
             )
 
         def chain_h_sq(i):
-            nc.vector.tensor_scalar(
+            engine = nc.vector if i < PLAIN else nc.gpsimd
+            engine.tensor_scalar(
                 out=col(h_sq, i), in0=h_sq_parts[:, i, 0:1], scalar1=h_sq_parts[:, i, 1:2], scalar2=MIN_SQ,
                 op0=ALU.add, op1=ALU.max,
             )
@@ -537,14 +540,14 @@ def tile_hyperboliclinearhyperboloid_kernel(tc, x, weight_words, weight_scales, 
             sum_h_squared(q, 0)
             exponentials(q - 1)
             sum_h_squared(q, 1)
+            chain_h_sq(q)
+            chain_r_inv(q)
             chain_y(q - 1)
             if q + 3 < TILES:
                 regroup(q + 3)
             chain_x(q - 1)
             finish(q - 2, 0)
             finish(q - 2, 1)
-            chain_h_sq(q)
-            chain_r_inv(q)
             if q + 2 < TILES:
                 quantise(q + 2)
             multiply_half(q + 1, 1)

from contextlib import ExitStack

import concourse.mybir as mybir
from concourse.masks import make_identity

F32 = mybir.dt.float32
BF16 = mybir.dt.bfloat16
I32 = mybir.dt.int32
U32 = mybir.dt.uint32
U8 = mybir.dt.uint8
FP8X4 = mybir.dt.float8_e4m3fn_x4
ALU = mybir.AluOpType
ACT = mybir.ActivationFunctionType

P = 128
ROWS = 2048
K = 1024
N = 1024
K_PASS = 512
PASSES = K // K_PASS
BANK = 512
HALVES = N // BANK
TILES = ROWS // P
ROW_RUN = 8
BLOCKS = TILES // ROW_RUN
O_ROW = N + 1
O_RUN = ROW_RUN * O_ROW
HALF_WAY = (ROW_RUN - 1) * O_ROW + 1 + BANK
X_PITCH = 1040
V_COPIES = (4,)
OWN_INPUTS = 8
PLAIN = 2
BEFORE_W = 5
V_SQUARES = (3, 5, 6)
WHOLE = 2

EPS = 1e-7
MIN_SQ = 1e-30
MAX_ARG = 15.0

FLOPS = 2 * ROWS * K * N


def col(tile, i):
    return tile[:, i : i + 1]


def tile_hyperboliclinearhyperboloid_kernel(tc, x, weight_words, weight_scales, bias, out):
    nc = tc.nc
    with ExitStack() as ctx:
        keep = ctx.enter_context(tc.tile_pool(name="keep", bufs=1))
        work = ctx.enter_context(tc.tile_pool(name="work", bufs=3))
        junk = ctx.enter_context(tc.tile_pool(name="junk", bufs=2))
        turn = ctx.enter_context(tc.psum_pool(name="turn", bufs=1))
        prod = ctx.enter_context(tc.psum_pool(name="prod", bufs=7))
        ctx.enter_context(tc.manual_schedule())

        half = keep.tile([P, TILES], F32)
        nc.vector.memset(half[:], 0.5)
        neg_half = keep.tile([P, TILES], F32)
        nc.vector.memset(neg_half[:], -0.5)
        w_codes = keep.tile([P, PASSES, N], U32, align_bytes=64)
        w_scales = keep.tile([P, N], U8, align_bytes=64)
        nc.vector.memset(w_scales[:].bitcast(I32), 0)
        ident = keep.tile([P, P], F32)
        make_identity(nc, ident[:])

        x_all = keep.tile([P, TILES, X_PITCH], BF16)
        x_time = keep.tile([P, BLOCKS, 2 * ROW_RUN], BF16)
        b_rows = keep.tile([P, N], BF16)

        def spatial(i):
            if i < WHOLE:
                return x_all[:, i, 1 : K + 1]
            return x_all[:, i, 0:K]

        x_tiles = x.rearrange("(s p j) c -> s j p c", p=P, j=ROW_RUN)

        def load_rows(i):
            rows = x_tiles[i // ROW_RUN][i % ROW_RUN]
            if i < WHOLE:
                nc.sync.dma_start(out=x_all[:, i, 0 : K + 1], in_=rows)
            else:
                nc.sync.dma_start(out=x_all[:, i, 0:K], in_=rows[:, 1 : K + 1])

        for i in range(WHOLE):
            load_rows(i)
        with nc.allow_non_contiguous_dma(reason="one bfloat16 element of each row of x"):
            for s in range(BLOCKS):
                j0 = WHOLE if s == 0 else 0
                nc.sync.dma_start(
                    out=x_time[:, s, j0:ROW_RUN],
                    in_=x_tiles[s][j0:ROW_RUN, :, 0:1].rearrange("j p o -> p (j o)"),
                )
        nc.sync.dma_start(out=b_rows[:], in_=bias.rearrange("o n -> (o n)").partition_broadcast(P))
        for i in range(WHOLE, BEFORE_W):
            load_rows(i)
        for g in range(PASSES):
            nc.sync.dma_start(
                out=w_codes[:, g, :].bitcast(I32),
                in_=weight_words[g].rearrange("p n t -> p (n t)").bitcast(I32),
            )
        for quad in range(4):
            nc.sync.dma_start(
                out=w_scales[32 * quad : 32 * quad + 4 * PASSES, :].bitcast(I32),
                in_=weight_scales[:, 4 * quad : 4 * quad + 4, :].bitcast(I32),
            )
        for i in range(BEFORE_W, TILES):
            load_rows(i)

        u_codes = keep.tile([P, TILES, PASSES * P], U32, align_bytes=64)
        u_scales = keep.tile([P, TILES, PASSES * P], U8, align_bytes=64)
        o_all = keep.tile([P, BLOCKS, O_RUN], F32)
        out_runs = out.rearrange("(s p j) c -> s p (j c)", p=P, j=ROW_RUN)

        sp_sq = keep.tile([P, TILES], F32)
        sp_sq_min = keep.tile([P, TILES], F32)
        inv_norm = keep.tile([P, TILES], F32)
        h_sq_parts = keep.tile([P, TILES, HALVES], F32)
        h_b_parts = keep.tile([P, TILES, HALVES], F32)
        h_sq = keep.tile([P, TILES], F32)
        r_inv = keep.tile([P, TILES], F32)
        r_arg = keep.tile([P, TILES], F32)
        along = keep.tile([P, TILES], F32)
        x_fac = keep.tile([P, TILES], F32)
        y_fac = keep.tile([P, TILES], F32)
        shift = keep.tile([P, TILES], F32)
        r_exp = keep.tile([P, TILES], F32)
        r_exp_neg = keep.tile([P, TILES], F32)
        y_neg = keep.tile([P, TILES], F32)
        x_less_y = keep.tile([P, TILES], F32)
        x_less_shift = keep.tile([P, TILES], F32)
        x_alone = keep.tile([P, TILES], F32)
        coef = keep.tile([P, TILES], F32)
        z_sq = keep.tile([P, TILES], F32)
        time_sq = keep.tile([P, TILES], F32)
        time_co = keep.tile([P, TILES], F32)

        u_of = {}
        turned_of = {}
        grouped_of = {}
        bank_of = {}

        def square_rows(i):
            sp = spatial(i)
            if i in V_SQUARES:
                sq_v = junk.tile([P, K], F32)
                nc.vector.scalar_tensor_tensor(
                    out=sq_v[:], in0=sp, scalar=1.0, in1=sp, op0=ALU.mult, op1=ALU.mult, accum_out=col(sp_sq, i)
                )
            else:
                sq_s = junk.tile([P, K], BF16)
                nc.scalar.activation(out=sq_s[:], in_=sp, func=ACT.Square, accum_out=col(sp_sq, i))

        def clamp_squares(i, n):
            cols = slice(i, i + n)
            engine = nc.vector if i < OWN_INPUTS else nc.gpsimd
            engine.tensor_scalar(out=sp_sq_min[:, cols], in0=sp_sq[:, cols], scalar1=MIN_SQ, scalar2=None, op0=ALU.max)

        def inverse_roots(i, n):
            cols = slice(i, i + n)
            nc.gpsimd.tensor_tensor(out=inv_norm[:, cols], in0=sp_sq_min[:, cols], in1=neg_half[:, 0:n], op=ALU.pow)

        def scale_rows(i):
            u_bf = work.tile([P, K], BF16, align_bytes=64)
            nc.vector.tensor_scalar(
                out=u_bf[:], in0=spatial(i), scalar1=col(inv_norm, i), scalar2=col(dist, i), op0=ALU.mult, op1=ALU.mult
            )
            u_of[i] = u_bf

        def turn_rows(i):
            if i == 1:
                h_bank = prod.tile([P, BANK], F32)
                turned = h_bank[:].rearrange("p (g w r) -> p g w r", g=PASSES, w=2)
            else:
                t_bank = turn.tile([P, BANK], F32)
                turned = t_bank[:].rearrange("p (g w r) -> p g w r", g=PASSES, w=2)
            u_words = u_of[i][:].bitcast(F32)
            for g in range(PASSES):
                for w in range(2):
                    nc.tensor.transpose(turned[:, g, w, :], u_words[:, 256 * g + w : 256 * (g + 1) : 2], ident[:])
            turned_of[i] = turned

        def regroup(i):
            grouped = work.tile([P, PASSES * P * 4], BF16, align_bytes=64)
            copy = nc.vector.tensor_copy if i in V_COPIES else nc.scalar.copy
            copy(
                out=grouped[:].bitcast(F32).rearrange("p (g r w) -> p g r w", g=PASSES, w=2),
                in_=turned_of[i].rearrange("p g w r -> p g r w"),
            )
            grouped_of[i] = grouped

        def quantise(i):
            nc.vector.quantize_mx(out=u_codes[:, i, :].bitcast(FP8X4), scales=u_scales[:, i, :], in_=grouped_of[i][:])

        def multiply_half(i, nh):
            h_bank = prod.tile([P, BANK], F32)
            n_cols = slice(nh * BANK, (nh + 1) * BANK)
            for g in range(PASSES):
                m_cols = slice(g * P, (g + 1) * P)
                nc.tensor.matmul_mx(
                    out=h_bank[:],
                    lhsT=u_codes[:, i, m_cols].bitcast(FP8X4),
                    lhsT_scale=u_scales[:, i, m_cols],
                    rhs=w_codes[:, g, n_cols].bitcast(FP8X4),
                    rhs_scale=w_scales[4 * g : P, n_cols],
                    start=(g == 0),
                    stop=(g == PASSES - 1),
                )
            bank_of[(i, nh)] = h_bank

        def multiply(i):
            for nh in range(HALVES):
                multiply_half(i, nh)

        def sum_h_bias(i, nh):
            hb_junk = junk.tile([P, BANK], F32)
            nc.vector.scalar_tensor_tensor(
                out=hb_junk[:], in0=bank_of[(i, nh)][:], scalar=1.0 if i < PLAIN else st[:, 0:1],
                in1=b_rows[:, nh * BANK : (nh + 1) * BANK],
                op0=ALU.mult, op1=ALU.mult, accum_out=h_b_parts[:, i, nh : nh + 1],
            )

        def sum_h_squared(i, nh):
            hh_junk = junk.tile([P, BANK], BF16)
            nc.scalar.activation(
                out=hh_junk[:], in_=bank_of[(i, nh)][:], func=ACT.Square, accum_out=h_sq_parts[:, i, nh : nh + 1]
            )

        def chain_h_sq(i):
            engine = nc.vector if i < PLAIN else nc.gpsimd
            engine.tensor_scalar(
                out=col(h_sq, i), in0=h_sq_parts[:, i, 0:1], scalar1=h_sq_parts[:, i, 1:2], scalar2=MIN_SQ,
                op0=ALU.add, op1=ALU.max,
            )

        def chain_r_inv(i):
            nc.gpsimd.tensor_tensor(out=col(r_inv, i), in0=col(h_sq, i), in1=neg_half[:, 0:1], op=ALU.pow)

        def chain_after_r_inv(i):
            nc.vector.tensor_scalar(
                out=col(r_arg, i), in0=col(h_sq, i), scalar1=col(r_inv, i), scalar2=MAX_ARG, op0=ALU.mult, op1=ALU.min
            )
            nc.vector.tensor_scalar(
                out=col(along, i), in0=h_b_parts[:, i, 0:1], scalar1=h_b_parts[:, i, 1:2], scalar2=col(r_inv, i),
                op0=ALU.add, op1=ALU.mult,
            )

        def shift_of(i):
            return col(shift, i) if i < PLAIN else col(along, i)

        def exponentials(i):
            half_of = half_st[:, 0:1] if i < PLAIN else 0.5
            nc.scalar.activation(out=col(r_exp, i), in_=col(r_arg, i), func=ACT.Exp)
            nc.scalar.activation(out=col(r_exp_neg, i), in_=col(r_arg, i), func=ACT.Exp, scale=-1.0)
            nc.scalar.activation(
                out=col(y_fac, i), in_=col(along, i), func=ACT.Identity, scale=half_of, bias=neg_half_ct[:, 0:1]
            )
            nc.scalar.activation(
                out=col(x_fac, i), in_=col(along, i), func=ACT.Identity, scale=half_of, bias=half_ct[:, 0:1]
            )
            if i < PLAIN:
                nc.scalar.activation(out=col(shift, i), in_=col(along, i), func=ACT.Identity, scale=st[:, 0:1])

        def chain_y(i):
            nc.scalar.activation(out=col(y_neg, i), in_=col(r_exp_neg, i), func=ACT.Identity, scale=col(y_fac, i))

        def chain_x(i):
            nc.scalar.activation(
                out=col(x_less_y, i), in_=col(r_exp, i), func=ACT.Identity, scale=col(x_fac, i), bias=col(y_neg, i)
            )

        def chain_coef(i):
            nc.vector.tensor_scalar(
                out=col(coef, i), in0=col(x_less_y, i), scalar1=shift_of(i), scalar2=col(r_inv, i),
                op0=ALU.subtract, op1=ALU.mult,
            )

        def chain_pair(i):
            nc.vector.tensor_scalar(
                out=col(y_neg, i), in0=col(r_exp_neg, i), scalar1=col(y_fac, i), scalar2=None, op0=ALU.mult
            )
            nc.vector.tensor_scalar(
                out=col(x_less_shift, i), in0=col(r_exp, i), scalar1=col(x_fac, i), scalar2=shift_of(i),
                op0=ALU.mult, op1=ALU.subtract,
            )
            nc.vector.tensor_scalar(
                out=col(x_alone, i), in0=col(r_exp, i), scalar1=col(x_fac, i), scalar2=None, op0=ALU.mult
            )

        def chain_coef_of_pair(i):
            nc.vector.tensor_scalar(
                out=col(coef, i), in0=col(x_less_shift, i), scalar1=col(y_neg, i), scalar2=col(r_inv, i),
                op0=ALU.add, op1=ALU.mult,
            )

        def chain_z_sq_of_pair(i):
            nc.scalar.activation(out=col(z_sq, i), in_=col(y_neg, i), func=ACT.Square, scale=-1.0, bias=col(x_alone, i))

        def chain_z_sq(i):
            nc.scalar.activation(
                out=col(z_sq, i), in_=col(y_neg, i), func=ACT.Square, scale=-2.0, bias=col(x_less_y, i)
            )

        def time_squares(i, n):
            cols = slice(i, i + n)
            nc.scalar.activation(out=time_sq[:, cols], in_=z_sq[:, cols], func=ACT.Identity, bias=delta_one[:, 0:1])

        def time_roots(i, n):
            cols = slice(i, i + n)
            nc.gpsimd.tensor_tensor(out=time_co[:, cols], in0=time_sq[:, cols], in1=half[:, 0:n], op=ALU.pow)

        def place_times(i, n):
            nc.scalar.copy(
                out=o_all[:].rearrange("p s c -> p (s c)")[:, i * O_ROW : (i + n - 1) * O_ROW + 1 : O_ROW],
                in_=time_co[:, i : i + n],
            )

        def finish(i, nh):
            nc.vector.scalar_tensor_tensor(
                out=o_all[:, i // ROW_RUN, (i % ROW_RUN) * O_ROW + 1 + nh * BANK : (i % ROW_RUN) * O_ROW + 1 + (nh + 1) * BANK],
                in0=bank_of[(i, nh)][:],
                scalar=col(coef, i),
                in1=b_term[:, nh * BANK : (nh + 1) * BANK],
                op0=ALU.mult,
                op1=ALU.add,
            )

        def store_run(s, a, b):
            nc.sync.dma_start(out=out_runs[s][:, a:b], in_=o_all[:, s, a:b])

        def store(i):
            s, j = i // ROW_RUN, i % ROW_RUN
            store_run(s, N * j, O_RUN if j == ROW_RUN - 1 else N * (j + 1))


        theta = keep.tile([P, TILES], F32)
        theta_less = keep.tile([P, TILES], F32)
        below = keep.tile([P, TILES], F32)
        root = keep.tile([P, TILES], F32)
        ln_arg = keep.tile([P, TILES], F32)
        dist = keep.tile([P, TILES], F32)

        def clamp_times(a, b, times):
            nc.vector.tensor_scalar(out=theta[:, a:b], in0=times, scalar1=1.0 + EPS, scalar2=None, op0=ALU.max)
            nc.vector.tensor_scalar(out=theta_less[:, a:b], in0=times, scalar1=1.0 + EPS, scalar2=-1.0, op0=ALU.max, op1=ALU.add)

        def distance_start(a, b):
            nc.vector.scalar_tensor_tensor(
                out=below[:, a:b], in0=theta[:, a:b], scalar=1.0, in1=theta_less[:, a:b], op0=ALU.add, op1=ALU.mult
            )

        def distance_root(a, b):
            nc.gpsimd.tensor_tensor(out=root[:, a:b], in0=below[:, a:b], in1=half[:, a:b], op=ALU.pow)

        def distance_sum(a, b):
            nc.vector.tensor_tensor(out=ln_arg[:, a:b], in0=theta[:, a:b], in1=root[:, a:b], op=ALU.add)

        def distance_end(a, b):
            nc.scalar.activation(out=dist[:, a:b], in_=ln_arg[:, a:b], func=ACT.Ln)

        b_sq = keep.tile([P, 1], F32)
        b_sq_min = keep.tile([P, 1], F32)
        t_raw = keep.tile([P, 1], F32)
        t_arg = keep.tile([P, 1], F32)
        t_inv = keep.tile([P, 1], F32)
        t_exp = keep.tile([P, 1], F32)
        t_exp_neg = keep.tile([P, 1], F32)
        half_ct = keep.tile([P, 1], F32)
        neg_half_ct = keep.tile([P, 1], F32)
        two_st = keep.tile([P, 1], F32)
        half_st = keep.tile([P, 1], F32)
        st = keep.tile([P, 1], F32)
        neg_ct_sq = keep.tile([P, 1], F32)
        four_st_sq_bb = keep.tile([P, 1], F32)
        delta = keep.tile([P, 1], F32)
        delta_one = keep.tile([P, 1], F32)
        b_term = keep.tile([P, N], F32)

        def bias_first():
            nc.vector.tensor_scalar(
                out=half_ct[:], in0=t_exp[:], scalar1=t_exp_neg[:, 0:1], scalar2=0.25, op0=ALU.add, op1=ALU.mult
            )
            nc.vector.tensor_scalar(
                out=two_st[:], in0=t_exp[:], scalar1=t_exp_neg[:, 0:1], scalar2=t_inv[:, 0:1],
                op0=ALU.subtract, op1=ALU.mult,
            )

        def bias_second():
            nc.vector.tensor_scalar(out=neg_half_ct[:], in0=half_ct[:], scalar1=-1.0, scalar2=None, op0=ALU.mult)
            nc.vector.tensor_scalar(out=half_st[:], in0=two_st[:], scalar1=0.25, scalar2=None, op0=ALU.mult)
            nc.vector.tensor_scalar(out=st[:], in0=two_st[:], scalar1=0.5, scalar2=None, op0=ALU.mult)
            nc.vector.tensor_scalar(
                out=neg_ct_sq[:], in0=half_ct[:], scalar1=half_ct[:, 0:1], scalar2=-4.0, op0=ALU.mult, op1=ALU.mult
            )
            nc.vector.tensor_scalar(
                out=four_st_sq_bb[:], in0=two_st[:], scalar1=two_st[:, 0:1], scalar2=b_sq[:, 0:1],
                op0=ALU.mult, op1=ALU.mult,
            )

        def bias_third():
            nc.vector.tensor_scalar(
                out=delta[:], in0=four_st_sq_bb[:], scalar1=0.25, scalar2=neg_ct_sq[:, 0:1], op0=ALU.mult, op1=ALU.add
            )

        def bias_fourth():
            nc.vector.tensor_scalar(out=delta_one[:], in0=delta[:], scalar1=1.0, scalar2=None, op0=ALU.add)

        def bias_row():
            nc.vector.tensor_scalar(
                out=b_term[:], in0=b_rows[:], scalar1=two_st[:, 0:1], scalar2=0.5, op0=ALU.mult, op1=ALU.mult
            )

        warm = keep.tile([P, 1], F32)
        nc.scalar.activation(out=warm[:], in_=half[:, 0:1], func=ACT.Ln)
        square_rows(0)
        clamp_times(0, 1, x_all[:, 0:1, 0])
        distance_start(0, 1)
        distance_root(0, 1)
        clamp_times(1, 2, x_all[:, 1:2, 0])
        clamp_times(2, ROW_RUN, x_time[:, 0, 2:ROW_RUN])
        clamp_times(ROW_RUN, TILES, x_time[:, 1, 0:ROW_RUN])
        clamp_squares(0, 1)
        inverse_roots(0, 1)
        distance_start(1, TILES)
        square_rows(1)
        distance_sum(0, 1)
        distance_end(0, 1)
        distance_root(1, 6)
        square_rows(2)
        h_bank = prod.tile([P, BANK], F32)
        t_bank = turn.tile([P, BANK], F32)
        for repeat in range(5):
            nc.tensor.matmul(out=t_bank[:], lhsT=x_all[:, 0, 0:P], rhs=x_all[:, 0, P : P + BANK], start=True, stop=True)
        scale_rows(0)
        turn_rows(0)
        for repeat in range(3):
            nc.tensor.matmul(out=h_bank[:], lhsT=x_all[:, 0, 0:P], rhs=x_all[:, 0, P : P + BANK], start=True, stop=True)
        clamp_squares(1, 1)
        inverse_roots(1, 1)
        square_rows(3)
        distance_sum(1, 6)
        distance_end(1, 6)
        distance_root(6, TILES)
        clamp_squares(2, 2)
        inverse_roots(2, 2)
        scale_rows(1)
        turn_rows(1)
        regroup(0)
        quantise(0)
        multiply(0)
        square_rows(4)
        b_junk = junk.tile([P, N], F32)
        nc.vector.scalar_tensor_tensor(
            out=b_junk[:], in0=b_rows[:], scalar=1.0, in1=b_rows[:], op0=ALU.mult, op1=ALU.mult, accum_out=b_sq[:]
        )
        regroup(1)
        distance_sum(6, TILES)
        distance_end(6, TILES)
        nc.vector.tensor_scalar(out=b_sq_min[:], in0=b_sq[:], scalar1=1e-15, scalar2=None, op0=ALU.max)
        nc.gpsimd.tensor_tensor(out=t_raw[:], in0=b_sq_min[:], in1=half[:, 0:1], op=ALU.pow)
        nc.scalar.activation(out=warm[:], in_=half[:, 0:1], func=ACT.Exp)
        sum_h_bias(0, 0)
        quantise(1)
        sum_h_bias(0, 1)
        multiply(1)
        scale_rows(2)
        turn_rows(2)
        nc.vector.tensor_scalar(out=t_arg[:], in0=t_raw[:], scalar1=1e-15, scalar2=MAX_ARG, op0=ALU.max, op1=ALU.min)
        clamp_squares(4, 1)
        inverse_roots(4, 1)
        scale_rows(3)
        nc.vector.reciprocal(out=t_inv[:], in_=t_arg[:])
        nc.scalar.activation(out=t_exp[:], in_=t_arg[:], func=ACT.Exp)
        nc.scalar.activation(out=t_exp_neg[:], in_=t_arg[:], func=ACT.Exp, scale=-1.0)
        sum_h_squared(0, 0)
        sum_h_squared(0, 1)
        regroup(2)
        turn_rows(3)
        square_rows(5)
        chain_h_sq(0)
        chain_r_inv(0)
        bias_first()
        sum_h_bias(1, 0)
        bias_second()
        sum_h_bias(1, 1)
        bias_third()
        quantise(2)
        multiply(2)
        bias_fourth()
        scale_rows(4)
        clamp_squares(5, 1)
        inverse_roots(5, 1)
        chain_after_r_inv(0)
        square_rows(6)
        sum_h_squared(1, 0)
        sum_h_squared(1, 1)
        regroup(3)
        turn_rows(4)
        exponentials(0)
        square_rows(7)
        chain_h_sq(1)
        chain_r_inv(1)
        bias_row()
        quantise(3)
        clamp_squares(6, 2)
        inverse_roots(6, 2)
        chain_y(0)
        regroup(4)
        chain_x(0)

        def time_group_ending_at(i):
            if i < 0 or i >= TILES:
                return None
            if i == 0 or i >= TILES - 3:
                return (i, 1)
            if i % 2 == 0:
                return (i - 1, 2)
            return None

        for q in range(2, TILES - 1):
            multiply_half(q + 1, 0)
            if q + 3 < TILES:
                scale_rows(q + 3)
                turn_rows(q + 3)
            sum_h_bias(q, 0)
            chain_coef(q - 2)
            sum_h_bias(q, 1)
            chain_after_r_inv(q - 1)
            if q + 6 < TILES:
                square_rows(q + 6)
            chain_z_sq(q - 2)
            group = time_group_ending_at(q - 2)
            if group is not None:
                time_squares(group[0], group[1])
                time_roots(group[0], group[1])
            if q + 6 < TILES and (q + 6) % 2 == 1:
                clamp_squares(q + 5, 2)
                inverse_roots(q + 5, 2)
            sum_h_squared(q, 0)
            exponentials(q - 1)
            sum_h_squared(q, 1)
            chain_h_sq(q)
            chain_r_inv(q)
            chain_y(q - 1)
            if q + 3 < TILES:
                regroup(q + 3)
            chain_x(q - 1)
            finish(q - 2, 0)
            finish(q - 2, 1)
            if q + 2 < TILES:
                quantise(q + 2)
            multiply_half(q + 1, 1)
            if group is not None:
                place_times(group[0], group[1])
                for i in range(group[0], group[0] + group[1]):
                    store(i)

        last = TILES - 1
        sum_h_bias(last, 0)
        chain_coef(last - 2)
        sum_h_bias(last, 1)
        chain_after_r_inv(last - 1)
        chain_z_sq(last - 2)
        time_squares(last - 2, 1)
        time_roots(last - 2, 1)
        sum_h_squared(last, 0)
        exponentials(last - 1)
        sum_h_squared(last, 1)
        finish(last - 2, 0)
        chain_pair(last - 1)
        finish(last - 2, 1)
        chain_coef_of_pair(last - 1)
        chain_h_sq(last)
        chain_r_inv(last)
        place_times(last - 2, 1)
        store(last - 2)
        chain_z_sq_of_pair(last - 1)
        time_squares(last - 1, 1)
        time_roots(last - 1, 1)
        finish(last - 1, 0)
        finish(last - 1, 1)
        chain_after_r_inv(last)
        exponentials(last)
        place_times(last - 1, 1)
        store(last - 1)
        chain_pair(last)
        chain_coef_of_pair(last)
        chain_z_sq_of_pair(last)
        time_squares(last, 1)
        time_roots(last, 1)
        finish(last, 1)
        store_run(BLOCKS - 1, HALF_WAY, O_RUN)
        finish(last, 0)
        place_times(last, 1)
        store_run(BLOCKS - 1, N * (ROW_RUN - 1), HALF_WAY)
